import numpy as np
import ml_dtypes


def mxq(x, axis, fmt="e4m3"):
    dtype, down = {"e4m3": (ml_dtypes.float8_e4m3fn, 7), "e5m2": (ml_dtypes.float8_e5m2, 14)}[fmt]
    v = np.moveaxis(np.asarray(x, np.float32).astype(ml_dtypes.bfloat16).astype(np.float64), axis, -1)
    blocks = v.reshape(v.shape[:-1] + (-1, 32))
    amax = np.abs(blocks).max(-1, keepdims=True)
    byte = np.maximum(np.where(amax > 0, np.frexp(amax)[1] - 1 + 127, 0) - down, 1)
    scale = np.exp2(byte - 127.0)
    codes = (blocks / scale).astype(np.float32).astype(dtype).astype(np.float64)
    return np.moveaxis((codes * scale).reshape(v.shape), -1, axis)


WIDE = False


def mx_kscale(k):
    if not WIDE:
        return np.ones(k)
    levels = np.array([10, -10, 5, -5, 0])
    a = np.random.permutation(np.resize(levels, k // 512 * 4)).reshape(k // 512, 4)
    idx = np.arange(k)
    return np.exp2(a[idx // 512, idx % 128 // 32])


BF16 = ml_dtypes.bfloat16


def bf(x):
    return np.asarray(x, np.float32).astype(BF16)


def f64(x):
    return np.asarray(x).astype(np.float64)


N, D, N_BRANCH, N_OUT = 8192, 512, 1024, 128
BLOCK = N_BRANCH // 4


def erf(v):
    a = np.minimum(np.abs(v), 6.0)
    term = a.copy()
    total = a.copy()
    for n in range(1, 120):
        term = term * (2.0 * a * a) / (2 * n + 1)
        total = total + term
    return np.sign(v) * 2.0 / np.sqrt(np.pi) * np.exp(-a * a) * total


def _branch_activations(h):
    return np.concatenate([
        np.maximum(h[:, 0 * BLOCK:1 * BLOCK], 0.0),
        np.tanh(h[:, 1 * BLOCK:2 * BLOCK]),
        1.0 / (1.0 + np.exp(-h[:, 2 * BLOCK:3 * BLOCK])),
        0.5 * h[:, 3 * BLOCK:4 * BLOCK] * (1.0 + erf(h[:, 3 * BLOCK:4 * BLOCK] / np.sqrt(2.0))),
    ], axis=-1)


def setup_inputs():
    s = mx_kscale(D)
    t = np.ones(N_BRANCH)
    t[:BLOCK] = mx_kscale(N_BRANCH)[:BLOCK]
    return {"x": bf(np.random.standard_normal((N, D)) * s),
            "W": bf(np.random.standard_normal((D, N_BRANCH)) * 1.0 / np.sqrt(D) / s[:, None] * t),
            "b": bf(np.random.standard_normal(N_BRANCH) * 0.3 * t),
            "agg": bf(np.random.standard_normal((N_BRANCH, N_OUT)) * 1.5 / np.sqrt(N_BRANCH) / t[:, None])}


def reference(x, W, b, agg):
    h = (mxq(f64(x), 1, "e4m3") @ mxq(f64(W), 0, "e4m3")) + f64(b)
    concatenated = _branch_activations(h)
    return mxq(concatenated, 1, "e4m3") @ mxq(f64(agg), 0, "e4m3")

@@ -1,0 +1,297 @@
+from contextlib import ExitStack
+
+import concourse.mybir as mybir
+from concourse.masks import make_identity
+
+F32 = mybir.dt.float32
+BF16 = mybir.dt.bfloat16
+U32 = mybir.dt.uint32
+U8 = mybir.dt.uint8
+FP8X4 = mybir.dt.float8_e4m3fn_x4
+ACT = mybir.ActivationFunctionType
+ALU = mybir.AluOpType
+
+P = 128
+H = 64
+N_TOK = 8192
+D = 512
+N_BRANCH = 1024
+N_OUT = 128
+CH = 512
+N_CH = N_TOK // CH
+TPC = CH // P
+N_TT = N_TOK // P
+
+FLOPS = 2 * N_TOK * D * N_BRANCH + 2 * N_TOK * N_BRANCH * N_OUT
+
+
+def tile_kan_t_kernel(tc, x, W, b, agg, out):
+    nc = tc.nc
+    x_v = x.rearrange("(p i) k -> p i k", i=N_TT)
+    out_v = out.rearrange("(p i) o -> p i o", i=N_TT)
+
+    with ExitStack() as ctx:
+        keep = ctx.enter_context(tc.tile_pool(name="keep", bufs=1))
+        xpool = ctx.enter_context(tc.tile_pool(name="xraw", bufs=5))
+        gxpool = ctx.enter_context(tc.tile_pool(name="gx", bufs=3))
+        cqpool = ctx.enter_context(tc.tile_pool(name="cq", bufs=3))
+        gqpool = ctx.enter_context(tc.tile_pool(name="gq", bufs=3))
+        ccpool = ctx.enter_context(tc.tile_pool(name="cc", bufs=2))
+        opool = ctx.enter_context(tc.tile_pool(name="osb", bufs=3))
+        psa = ctx.enter_context(tc.psum_pool(name="psa", bufs=2))
+        psh = ctx.enter_context(tc.psum_pool(name="psh", bufs=6))
+        ctx.enter_context(tc.manual_schedule())
+
+        x_codes = keep.tile([P, N_TOK], U32, align_bytes=64)
+        x_scales = keep.tile([P, N_TOK], U8, align_bytes=64)
+        ts_codes = keep.tile([P, N_TOK], U32, align_bytes=64)
+        ts_scales = keep.tile([P, N_TOK], U8, align_bytes=64)
+        w_raw = keep.tile([P, 4, N_BRANCH], BF16)
+        w_grp = keep.tile([P, N_BRANCH, 4], BF16, align_bytes=64)
+        w_codes = keep.tile([P, N_BRANCH], U32, align_bytes=64)
+        w_scales = keep.tile([P, N_BRANCH], U8, align_bytes=64)
+        g_raw = keep.tile([P, 2, 4, N_OUT], BF16)
+        g_grp = keep.tile([P, 2, N_OUT, 4], BF16, align_bytes=64)
+        g_codes = keep.tile([P, 2, N_OUT], U32, align_bytes=64)
+        g_scales = keep.tile([P, 2, N_OUT], U8, align_bytes=64)
+        ident_f = keep.tile([P, P], F32)
+        ident_b = keep.tile([P, P], BF16)
+        b_rows = keep.tile([P, P], BF16)
+        bias_ts = keep.tile([P, 8], F32)
+        bm_raw = keep.tile([P, 4], BF16)
+        bias_mx = keep.tile([P, 4], F32)
+        warm = keep.tile([P, 2], F32)
+
+        xr = {}
+
+        def load_x(g):
+            xraw = xpool.tile([P, TPC, D], BF16)
+            nc.sync.dma_start(out=xraw[:], in_=x_v[:, TPC * g:TPC * (g + 1), :])
+            xr[g] = xraw
+
+        load_x(0)
+        for u in range(2):
+            nc.scalar.dma_start(
+                out=w_raw[:, 2 * u:2 * u + 2, :],
+                in_=W[256 * u:256 * (u + 1), :].rearrange("(q e) c -> q e c", e=2),
+            )
+        nc.vector.memset(warm[:], 0.0)
+        nc.vector.memset(b_rows[:], 0.0)
+        nc.scalar.dma_start(out=b_rows[0:8, :], in_=b.rearrange("(m c) -> m c", c=P))
+        nc.scalar.activation(out=warm[:, 1:2], in_=warm[:, 0:1], func=ACT.Sigmoid)
+        for g in range(1, 5):
+            load_x(g)
+        make_identity(nc, ident_f[:])
+        nc.gpsimd.dma_start(out=bm_raw[0:H, :], in_=b[0:256].rearrange("(p t) -> p t", t=4))
+        nc.gpsimd.dma_start(out=bm_raw[H:P, :], in_=b[768:1024].rearrange("(p t) -> p t", t=4))
+        nc.gpsimd.dma_start(out=g_raw[0:H, 0, :, :], in_=agg[0:256, :].rearrange("(p t) o -> p t o", t=4))
+        nc.gpsimd.dma_start(out=g_raw[H:P, 0, :, :], in_=agg[768:1024, :].rearrange("(p t) o -> p t o", t=4))
+        nc.gpsimd.dma_start(out=g_raw[:, 1, :, :], in_=agg[256:768, :].rearrange("(t p) o -> p t o", p=P))
+        nc.vector.tensor_copy(out=ident_b[:], in_=ident_f[:])
+
+        xts = {}
+        gxs = {}
+
+        def transposes(g):
+            x32 = xr[g][:].rearrange("p i k -> p (i k)").bitcast(F32)
+            banks = []
+            for a in range(2):
+                xt = psa.tile([P, 2, 2, P], F32, tag="a")
+                for i2 in range(2):
+                    for u in range(2):
+                        c0 = 256 * (2 * a + i2) + 128 * u
+                        nc.tensor.transpose(xt[:, i2, u, :], x32[:, c0:c0 + P], ident_f[:])
+                banks.append(xt)
+            xts[g] = banks
+
+        def x_evac(g, a):
+            if a == 0:
+                gx = gxpool.tile([P, CH, 4], BF16, align_bytes=64)
+                gxs[g] = gx
+            gx32 = gxs[g][:].rearrange("p r t -> p (r t)").bitcast(F32).rearrange("p (r u) -> p r u", u=2)
+            dst = gx32[:, 256 * a:256 * (a + 1), :].rearrange("p (i r) u -> p i r u", i=2)
+            src = xts[g][a][:].rearrange("p i u r -> p i r u")
+            if a == 0:
+                nc.scalar.copy(out=dst, in_=src)
+            else:
+                nc.vector.tensor_copy(out=dst, in_=src)
+
+        def x_quant(g):
+            cols = slice(CH * g, CH * (g + 1))
+            nc.vector.quantize_mx(
+                out=x_codes[:, cols].bitcast(FP8X4),
+                scales=x_scales[:, cols],
+                in_=gxs[g][:].rearrange("p r t -> p (r t)"),
+            )
+
+        def w_regroup_ts(j):
+            nc.vector.tensor_copy(
+                out=w_grp[:, 256 * j:256 * (j + 1), :].rearrange("p (c i) t -> p c t i", i=4),
+                in_=w_raw[:, :, 256 * (j + 1):256 * (j + 2)].rearrange("p t (c i) -> p c t i", i=4),
+            )
+
+        def w_regroup_mx(hf):
+            c0 = 768 * hf
+            nc.vector.tensor_copy(
+                out=w_grp[:, 512:1024, :].rearrange("p (t h j) k -> p t h j k", t=4, h=2)[:, :, hf, :, :],
+                in_=w_raw[:, :, c0:c0 + 256].rearrange("p k (j t) -> p t j k", t=4),
+            )
+
+        def w_quant(j):
+            cols = slice(256 * j, 256 * (j + 1))
+            nc.vector.quantize_mx(
+                out=w_codes[:, cols].bitcast(FP8X4),
+                scales=w_scales[:, cols],
+                in_=w_grp[:, cols, :].rearrange("p c t -> p (c t)"),
+            )
+
+        def mx1(g, m):
+            h = psh.tile([P, CH], F32, tag="h")
+            nc.tensor.matmul_mx(
+                out=h[:],
+                lhsT=w_codes[:, P * m:P * (m + 1)].bitcast(FP8X4),
+                lhsT_scale=w_scales[:, P * m:P * (m + 1)],
+                rhs=x_codes[:, CH * g:CH * (g + 1)].bitcast(FP8X4),
+                rhs_scale=x_scales[:, CH * g:CH * (g + 1)],
+                start=True,
+                stop=True,
+            )
+            return h
+
+        def interleave(dst, src):
+            nc.vector.tensor_copy(
+                out=dst.rearrange("p (c i) t -> p c t i", i=4),
+                in_=src.rearrange("p t (c i) -> p c t i", i=4),
+            )
+
+        def quant(codes, scales, grp):
+            nc.vector.quantize_mx(out=codes.bitcast(FP8X4), scales=scales,
+                                  in_=grp[:].rearrange("p r t -> p (r t)"))
+
+        bt = psa.tile([P, P], BF16, tag="a")
+        nc.tensor.transpose(bt[:], b_rows[:], ident_b[:])
+        nc.vector.tensor_copy(out=bias_ts[:], in_=bt[:, 0:8])
+        transposes(0)
+        x_evac(0, 0)
+        w_regroup_ts(0)
+        x_evac(0, 1)
+        w_regroup_ts(1)
+        w_quant(0)
+        x_quant(0)
+        w_quant(1)
+
+        cqs = {}
+        gqs = {}
+
+        def ilv(s):
+            gq = gqpool.tile([P, CH, 4], BF16, align_bytes=64)
+            interleave(gq[:], cqs[s][:])
+            gqs[s] = gq
+
+        def q_ts(s):
+            cols = slice(CH * s, CH * (s + 1))
+            quant(ts_codes[:, cols], ts_scales[:, cols], gqs[s])
+
+        for s in range(N_CH):
+            if s + 5 < N_CH:
+                load_x(s + 5)
+            if s + 1 < N_CH:
+                transposes(s + 1)
+                x_evac(s + 1, 0)
+            if s >= 1:
+                ilv(s - 1)
+            if s + 1 < N_CH:
+                x_evac(s + 1, 1)
+            if s >= 1:
+                q_ts(s - 1)
+            if s + 1 < N_CH:
+                x_quant(s + 1)
+            cq = cqpool.tile([P, 4, CH], BF16, tag="cq")
+            cqs[s] = cq
+            for t in range(4):
+                h = mx1(s, t)
+                nc.scalar.activation(out=cq[:, t, :], in_=h[:], func=(ACT.Tanh if t < 2 else ACT.Sigmoid),
+                                     bias=bias_ts[:, 2 + t:3 + t], scale=1.0)
+            if s == 1:
+                w_regroup_mx(0)
+                w_regroup_mx(1)
+                nc.vector.tensor_copy(out=bias_mx[:], in_=bm_raw[:])
+            if s == 2:
+                w_quant(2)
+                w_quant(3)
+                for q in range(2):
+                    nc.vector.tensor_copy(out=g_grp[:, q, :, :], in_=g_raw[:, q, :, :].rearrange("p t o -> p o t"))
+            if s == 3:
+                for q in range(2):
+                    nc.vector.quantize_mx(out=g_codes[:, q, :].bitcast(FP8X4), scales=g_scales[:, q, :],
+                                          in_=g_grp[:, q, :, :].rearrange("p o t -> p (o t)"))
+
+        hs = {}
+        ccs = {}
+        ops = {}
+
+        def mixed_mx(s, ts):
+            for t in ts:
+                hs[(s, t)] = mx1(s, 4 + t)
+
+        def mixed_evac(s):
+            cq = cqpool.tile([P, 4, CH], BF16, tag="cq")
+            cqs[s] = cq
+            for t in range(4):
+                h = hs[(s, t)]
+                nc.scalar.activation(out=cq[H:P, t, :], in_=h[H:P, :], func=ACT.Gelu,
+                                     bias=bias_mx[H:P, t:t + 1], scale=1.0)
+                if t < 2:
+                    nc.scalar.activation(out=cq[0:H, t, :], in_=h[0:H, :], func=ACT.Relu,
+                                         bias=bias_mx[0:H, t:t + 1], scale=1.0)
+                else:
+                    nc.vector.tensor_scalar(out=cq[0:H, t, :], in0=h[0:H, :], scalar1=bias_mx[0:H, t:t + 1],
+                                            scalar2=0.0, op0=ALU.add, op1=ALU.max)
+
+        def q_mx(s):
+            c_codes = ccpool.tile([P, CH], U32, align_bytes=64)
+            c_scales = ccpool.tile([P, CH], U8, align_bytes=64)
+            quant(c_codes[:], c_scales[:], gqs[s])
+            ccs[s] = (c_codes, c_scales)
+
+        def stage2(s):
+            c_codes, c_scales = ccs[s]
+            o_ps = psa.tile([P, TPC, N_OUT], F32, tag="a")
+            for j in range(TPC):
+                loc = slice(P * j, P * (j + 1))
+                glo = slice(CH * s + P * j, CH * s + P * (j + 1))
+                pairs = ((c_codes[:, loc], c_scales[:, loc]), (ts_codes[:, glo], ts_scales[:, glo]))
+                for q, (cod, sca) in enumerate(pairs):
+                    nc.tensor.matmul_mx(
+                        out=o_ps[:, j, :],
+                        lhsT=cod.bitcast(FP8X4),
+                        lhsT_scale=sca,
+                        rhs=g_codes[:, q, :].bitcast(FP8X4),
+                        rhs_scale=g_scales[:, q, :],
+                        start=(q == 0),
+                        stop=(q == 1),
+                    )
+            ops[s] = o_ps
+
+        def out_evac(s):
+            o_sb = opool.tile([P, TPC, N_OUT], F32)
+            nc.vector.tensor_copy(out=o_sb[:], in_=ops[s][:])
+            nc.sync.dma_start(out=out_v[:, TPC * s:TPC * (s + 1), :], in_=o_sb[:])
+
+        mixed_mx(0, (0, 1, 2, 3))
+        ilv(N_CH - 1)
+        q_ts(N_CH - 1)
+        for s in range(N_CH + 2):
+            if s + 1 < N_CH:
+                mixed_mx(s + 1, (0, 1))
+            if 1 <= s <= N_CH:
+                ilv(s - 1)
+            if s < N_CH:
+                mixed_evac(s)
+            if 1 <= s <= N_CH:
+                q_mx(s - 1)
+                stage2(s - 1)
+            if s + 1 < N_CH:
+                mixed_mx(s + 1, (2, 3))
+            if s >= 2:
+                out_evac(s - 2)

@@ -34,18 +34,18 @@ def tile_kan_t_kernel(tc, x, W, b, agg, out):
         keep = ctx.enter_context(tc.tile_pool(name="keep", bufs=1))
         xpool = ctx.enter_context(tc.tile_pool(name="xraw", bufs=5))
         gxpool = ctx.enter_context(tc.tile_pool(name="gx", bufs=3))
-        cqpool = ctx.enter_context(tc.tile_pool(name="cq", bufs=3))
+        cqpool = ctx.enter_context(tc.tile_pool(name="cq", bufs=5))
+        gepool = ctx.enter_context(tc.tile_pool(name="ge", bufs=4))
         gqpool = ctx.enter_context(tc.tile_pool(name="gq", bufs=3))
-        ccpool = ctx.enter_context(tc.tile_pool(name="cc", bufs=2))
+        ccpool = ctx.enter_context(tc.tile_pool(name="cc", bufs=3))
         opool = ctx.enter_context(tc.tile_pool(name="osb", bufs=3))
         psa = ctx.enter_context(tc.psum_pool(name="psa", bufs=2))
         psh = ctx.enter_context(tc.psum_pool(name="psh", bufs=6))
-        ctx.enter_context(tc.manual_schedule())
 
         x_codes = keep.tile([P, N_TOK], U32, align_bytes=64)
         x_scales = keep.tile([P, N_TOK], U8, align_bytes=64)
-        ts_codes = keep.tile([P, N_TOK], U32, align_bytes=64)
-        ts_scales = keep.tile([P, N_TOK], U8, align_bytes=64)
+        rg_codes = keep.tile([P, N_TOK], U32, align_bytes=64)
+        rg_scales = keep.tile([P, N_TOK], U8, align_bytes=64)
         w_raw = keep.tile([P, 4, N_BRANCH], BF16)
         w_grp = keep.tile([P, N_BRANCH, 4], BF16, align_bytes=64)
         w_codes = keep.tile([P, N_BRANCH], U32, align_bytes=64)
@@ -58,8 +58,10 @@ def tile_kan_t_kernel(tc, x, W, b, agg, out):
         ident_b = keep.tile([P, P], BF16)
         b_rows = keep.tile([P, P], BF16)
         bias_ts = keep.tile([P, 8], F32)
-        bm_raw = keep.tile([P, 4], BF16)
-        bias_mx = keep.tile([P, 4], F32)
+        bm_relu = keep.tile([P, 2, 2], BF16)
+        bm_gelu = keep.tile([P, 2, 2], BF16)
+        bms = (bm_relu, bm_gelu)
+        bias_rg = keep.tile([P, 2, 2], F32)
         warm = keep.tile([P, 2], F32)
 
         xr = {}
@@ -77,17 +79,24 @@ def tile_kan_t_kernel(tc, x, W, b, agg, out):
             )
         nc.vector.memset(warm[:], 0.0)
         nc.vector.memset(b_rows[:], 0.0)
-        nc.scalar.dma_start(out=b_rows[0:8, :], in_=b.rearrange("(m c) -> m c", c=P))
-        nc.scalar.activation(out=warm[:, 1:2], in_=warm[:, 0:1], func=ACT.Sigmoid)
+        for f in range(2):
+            for hf in range(2):
+                nc.gpsimd.dma_start(
+                    out=bms[f][H * hf:H * (hf + 1), :, :],
+                    in_=b[768 * f:768 * f + 256].rearrange("(p r h) -> p r h", r=2, h=2),
+                )
+        nc.scalar.activation(out=warm[:, 1:2], in_=warm[:, 0:1], func=ACT.Gelu)
         for g in range(1, 5):
             load_x(g)
         make_identity(nc, ident_f[:])
-        nc.gpsimd.dma_start(out=bm_raw[0:H, :], in_=b[0:256].rearrange("(p t) -> p t", t=4))
-        nc.gpsimd.dma_start(out=bm_raw[H:P, :], in_=b[768:1024].rearrange("(p t) -> p t", t=4))
+        nc.gpsimd.dma_start(out=b_rows[0:8, :], in_=b.rearrange("(m c) -> m c", c=P))
         nc.gpsimd.dma_start(out=g_raw[0:H, 0, :, :], in_=agg[0:256, :].rearrange("(p t) o -> p t o", t=4))
         nc.gpsimd.dma_start(out=g_raw[H:P, 0, :, :], in_=agg[768:1024, :].rearrange("(p t) o -> p t o", t=4))
         nc.gpsimd.dma_start(out=g_raw[:, 1, :, :], in_=agg[256:768, :].rearrange("(t p) o -> p t o", p=P))
-        nc.vector.tensor_copy(out=ident_b[:], in_=ident_f[:])
+        nc.vector.tensor_copy(out=bias_rg[0:H, 0, :], in_=bm_relu[0:H, :, 0])
+        nc.vector.tensor_copy(out=bias_rg[H:P, 0, :], in_=bm_relu[H:P, :, 1])
+        nc.vector.tensor_copy(out=bias_rg[0:H, 1, :], in_=bm_gelu[0:H, :, 1])
+        nc.vector.tensor_copy(out=bias_rg[H:P, 1, :], in_=bm_gelu[H:P, :, 0])
 
         xts = {}
         gxs = {}
@@ -104,17 +113,15 @@ def tile_kan_t_kernel(tc, x, W, b, agg, out):
                 banks.append(xt)
             xts[g] = banks
 
-        def x_evac(g, a):
-            if a == 0:
-                gx = gxpool.tile([P, CH, 4], BF16, align_bytes=64)
-                gxs[g] = gx
-            gx32 = gxs[g][:].rearrange("p r t -> p (r t)").bitcast(F32).rearrange("p (r u) -> p r u", u=2)
-            dst = gx32[:, 256 * a:256 * (a + 1), :].rearrange("p (i r) u -> p i r u", i=2)
-            src = xts[g][a][:].rearrange("p i u r -> p i r u")
-            if a == 0:
-                nc.scalar.copy(out=dst, in_=src)
-            else:
-                nc.vector.tensor_copy(out=dst, in_=src)
+        def x_evac(g):
+            gx = gxpool.tile([P, CH, 4], BF16, align_bytes=64)
+            gxs[g] = gx
+            gx32 = gx[:].rearrange("p r t -> p (r t)").bitcast(F32).rearrange("p (r u) -> p r u", u=2)
+            for a in range(2):
+                nc.scalar.copy(
+                    out=gx32[:, 256 * a:256 * (a + 1), :].rearrange("p (i r) u -> p i r u", i=2),
+                    in_=xts[g][a][:].rearrange("p i u r -> p i r u"),
+                )
 
         def x_quant(g):
             cols = slice(CH * g, CH * (g + 1))
@@ -124,17 +131,22 @@ def tile_kan_t_kernel(tc, x, W, b, agg, out):
                 in_=gxs[g][:].rearrange("p r t -> p (r t)"),
             )
 
-        def w_regroup_ts(j):
+        def w_regroup_relu():
             nc.vector.tensor_copy(
-                out=w_grp[:, 256 * j:256 * (j + 1), :].rearrange("p (c i) t -> p c t i", i=4),
-                in_=w_raw[:, :, 256 * (j + 1):256 * (j + 2)].rearrange("p t (c i) -> p c t i", i=4),
+                out=w_grp[:, 0:256, :].rearrange("p (t j) k -> p t j k", t=4),
+                in_=w_raw[:, :, 0:256].rearrange("p k (j t) -> p t j k", t=4),
             )
 
-        def w_regroup_mx(hf):
-            c0 = 768 * hf
+        def w_regroup_gelu(hf):
             nc.vector.tensor_copy(
-                out=w_grp[:, 512:1024, :].rearrange("p (t h j) k -> p t h j k", t=4, h=2)[:, :, hf, :, :],
-                in_=w_raw[:, :, c0:c0 + 256].rearrange("p k (j t) -> p t j k", t=4),
+                out=w_grp[:, 256:512, :].rearrange("p (r h j) k -> p r h j k", r=2, h=2)[:, :, hf, :, :],
+                in_=w_raw[:, :, 768:1024].rearrange("p k (j r g) -> p r g j k", r=2, g=2)[:, :, 1 - hf, :, :],
+            )
+
+        def w_regroup_ts(j):
+            nc.vector.tensor_copy(
+                out=w_grp[:, 256 * (j + 2):256 * (j + 3), :].rearrange("p (c i) t -> p c t i", i=4),
+                in_=w_raw[:, :, 256 * (j + 1):256 * (j + 2)].rearrange("p t (c i) -> p c t i", i=4),
             )
 
         def w_quant(j):
@@ -168,54 +180,50 @@ def tile_kan_t_kernel(tc, x, W, b, agg, out):
             nc.vector.quantize_mx(out=codes.bitcast(FP8X4), scales=scales,
                                   in_=grp[:].rearrange("p r t -> p (r t)"))
 
-        bt = psa.tile([P, P], BF16, tag="a")
-        nc.tensor.transpose(bt[:], b_rows[:], ident_b[:])
-        nc.vector.tensor_copy(out=bias_ts[:], in_=bt[:, 0:8])
         transposes(0)
-        x_evac(0, 0)
-        w_regroup_ts(0)
-        x_evac(0, 1)
-        w_regroup_ts(1)
+        x_evac(0)
+        w_regroup_relu()
+        w_regroup_gelu(0)
         w_quant(0)
+        w_regroup_gelu(1)
         x_quant(0)
         w_quant(1)
-
-        cqs = {}
-        gqs = {}
-
-        def ilv(s):
-            gq = gqpool.tile([P, CH, 4], BF16, align_bytes=64)
-            interleave(gq[:], cqs[s][:])
-            gqs[s] = gq
-
-        def q_ts(s):
-            cols = slice(CH * s, CH * (s + 1))
-            quant(ts_codes[:, cols], ts_scales[:, cols], gqs[s])
 
         for s in range(N_CH):
             if s + 5 < N_CH:
                 load_x(s + 5)
             if s + 1 < N_CH:
                 transposes(s + 1)
-                x_evac(s + 1, 0)
-            if s >= 1:
-                ilv(s - 1)
-            if s + 1 < N_CH:
-                x_evac(s + 1, 1)
-            if s >= 1:
-                q_ts(s - 1)
-            if s + 1 < N_CH:
+                x_evac(s + 1)
                 x_quant(s + 1)
-            cq = cqpool.tile([P, 4, CH], BF16, tag="cq")
-            cqs[s] = cq
-            for t in range(4):
-                h = mx1(s, t)
-                nc.scalar.activation(out=cq[:, t, :], in_=h[:], func=(ACT.Tanh if t < 2 else ACT.Sigmoid),
-                                     bias=bias_ts[:, 2 + t:3 + t], scale=1.0)
+            cq = cqpool.tile([P, 2, 2, CH], BF16, tag="cq")
+            ge = gepool.tile([P, 2, CH], BF16)
+            for r in range(2):
+                h = mx1(s, r)
+                if r == 0 or s % 2 == 1:
+                    nc.scalar.activation(out=cq[:, r, 0, :], in_=h[:], func=ACT.Relu,
+                                         bias=bias_rg[:, 0, r:r + 1], scale=1.0)
+                else:
+                    nc.vector.tensor_scalar(out=cq[:, r, 0, :], in0=h[:], scalar1=bias_rg[:, 0, r:r + 1],
+                                            scalar2=0.0, op0=ALU.add, op1=ALU.max)
+            nc.sync.dma_start(out=cq[0:H, :, 1, :], in_=cq[H:P, :, 0, :])
+            for r in range(2):
+                h = mx1(s, 2 + r)
+                nc.scalar.activation(out=ge[:, r, :], in_=h[:], func=ACT.Gelu,
+                                     bias=bias_rg[:, 1, r:r + 1], scale=1.0)
+            nc.sync.dma_start(out=cq[H:P, :, 1, :], in_=ge[0:H, :, :])
+            nc.vector.tensor_copy(out=cq[H:P, :, 0, :], in_=ge[H:P, :, :])
+            gq = gqpool.tile([P, CH, 4], BF16, align_bytes=64)
+            interleave(gq[:], cq[:].rearrange("p r h c -> p (r h) c"))
+            cols = slice(CH * s, CH * (s + 1))
+            quant(rg_codes[:, cols], rg_scales[:, cols], gq)
             if s == 1:
-                w_regroup_mx(0)
-                w_regroup_mx(1)
-                nc.vector.tensor_copy(out=bias_mx[:], in_=bm_raw[:])
+                nc.vector.tensor_copy(out=ident_b[:], in_=ident_f[:])
+                bt = psa.tile([P, P], BF16, tag="a")
+                nc.tensor.transpose(bt[:], b_rows[:], ident_b[:])
+                nc.vector.tensor_copy(out=bias_ts[:], in_=bt[:, 0:8])
+                w_regroup_ts(0)
+                w_regroup_ts(1)
             if s == 2:
                 w_quant(2)
                 w_quant(3)
@@ -226,41 +234,22 @@ def tile_kan_t_kernel(tc, x, W, b, agg, out):
                     nc.vector.quantize_mx(out=g_codes[:, q, :].bitcast(FP8X4), scales=g_scales[:, q, :],
                                           in_=g_grp[:, q, :, :].rearrange("p o t -> p (o t)"))
 
-        hs = {}
-        ccs = {}
-        ops = {}
-
-        def mixed_mx(s, ts):
-            for t in ts:
-                hs[(s, t)] = mx1(s, 4 + t)
-
-        def mixed_evac(s):
-            cq = cqpool.tile([P, 4, CH], BF16, tag="cq")
-            cqs[s] = cq
+        for s in range(N_CH):
+            ct = cqpool.tile([P, 4, CH], BF16, tag="cq")
             for t in range(4):
-                h = hs[(s, t)]
-                nc.scalar.activation(out=cq[H:P, t, :], in_=h[H:P, :], func=ACT.Gelu,
-                                     bias=bias_mx[H:P, t:t + 1], scale=1.0)
-                if t < 2:
-                    nc.scalar.activation(out=cq[0:H, t, :], in_=h[0:H, :], func=ACT.Relu,
-                                         bias=bias_mx[0:H, t:t + 1], scale=1.0)
-                else:
-                    nc.vector.tensor_scalar(out=cq[0:H, t, :], in0=h[0:H, :], scalar1=bias_mx[0:H, t:t + 1],
-                                            scalar2=0.0, op0=ALU.add, op1=ALU.max)
-
-        def q_mx(s):
+                h = mx1(s, 4 + t)
+                nc.scalar.activation(out=ct[:, t, :], in_=h[:], func=(ACT.Tanh if t < 2 else ACT.Sigmoid),
+                                     bias=bias_ts[:, 2 + t:3 + t], scale=1.0)
+            gq = gqpool.tile([P, CH, 4], BF16, align_bytes=64)
+            interleave(gq[:], ct[:])
             c_codes = ccpool.tile([P, CH], U32, align_bytes=64)
             c_scales = ccpool.tile([P, CH], U8, align_bytes=64)
-            quant(c_codes[:], c_scales[:], gqs[s])
-            ccs[s] = (c_codes, c_scales)
-
-        def stage2(s):
-            c_codes, c_scales = ccs[s]
+            quant(c_codes[:], c_scales[:], gq)
             o_ps = psa.tile([P, TPC, N_OUT], F32, tag="a")
             for j in range(TPC):
                 loc = slice(P * j, P * (j + 1))
                 glo = slice(CH * s + P * j, CH * s + P * (j + 1))
-                pairs = ((c_codes[:, loc], c_scales[:, loc]), (ts_codes[:, glo], ts_scales[:, glo]))
+                pairs = ((rg_codes[:, glo], rg_scales[:, glo]), (c_codes[:, loc], c_scales[:, loc]))
                 for q, (cod, sca) in enumerate(pairs):
                     nc.tensor.matmul_mx(
                         out=o_ps[:, j, :],
@@ -271,27 +260,6 @@ def tile_kan_t_kernel(tc, x, W, b, agg, out):
                         start=(q == 0),
                         stop=(q == 1),
                     )
-            ops[s] = o_ps
-
-        def out_evac(s):
             o_sb = opool.tile([P, TPC, N_OUT], F32)
-            nc.vector.tensor_copy(out=o_sb[:], in_=ops[s][:])
+            nc.vector.tensor_copy(out=o_sb[:], in_=o_ps[:])
             nc.sync.dma_start(out=out_v[:, TPC * s:TPC * (s + 1), :], in_=o_sb[:])
-
-        mixed_mx(0, (0, 1, 2, 3))
-        ilv(N_CH - 1)
-        q_ts(N_CH - 1)
-        for s in range(N_CH + 2):
-            if s + 1 < N_CH:
-                mixed_mx(s + 1, (0, 1))
-            if 1 <= s <= N_CH:
-                ilv(s - 1)
-            if s < N_CH:
-                mixed_evac(s)
-            if 1 <= s <= N_CH:
-                q_mx(s - 1)
-                stage2(s - 1)
-            if s + 1 < N_CH:
-                mixed_mx(s + 1, (2, 3))
-            if s >= 2:
-                out_evac(s - 2)

@@ -212,7 +212,7 @@ def tile_kan_t_kernel(tc, x, W, b, agg, out):
                 nc.scalar.activation(out=ge[:, r, :], in_=h[:], func=ACT.Gelu,
                                      bias=bias_rg[:, 1, r:r + 1], scale=1.0)
             nc.sync.dma_start(out=cq[H:P, :, 1, :], in_=ge[0:H, :, :])
-            nc.vector.tensor_copy(out=cq[H:P, :, 0, :], in_=ge[H:P, :, :])
+            nc.sync.dma_start(out=cq[H:P, :, 0, :], in_=ge[H:P, :, :])
             gq = gqpool.tile([P, CH, 4], BF16, align_bytes=64)
             interleave(gq[:], cq[:].rearrange("p r h c -> p (r h) c"))
             cols = slice(CH * s, CH * (s + 1))

@@ -24,6 +24,13 @@ N_TT = N_TOK // P
 
 FLOPS = 2 * N_TOK * D * N_BRANCH + 2 * N_TOK * N_BRANCH * N_OUT
 
+X_BUFS = 6
+LAG_MOVE = 4
+LAG_MM2 = 4
+S_RELU1 = (13, 14, 15)
+V_RELU0 = (0, 1, 2)
+S_OUT = (11, 12, 13, 14)
+
 
 def tile_kan_t_kernel(tc, x, W, b, agg, out):
     nc = tc.nc
@@ -32,15 +39,16 @@ def tile_kan_t_kernel(tc, x, W, b, agg, out):
 
     with ExitStack() as ctx:
         keep = ctx.enter_context(tc.tile_pool(name="keep", bufs=1))
-        xpool = ctx.enter_context(tc.tile_pool(name="xraw", bufs=5))
+        xpool = ctx.enter_context(tc.tile_pool(name="xraw", bufs=X_BUFS))
         gxpool = ctx.enter_context(tc.tile_pool(name="gx", bufs=3))
-        cqpool = ctx.enter_context(tc.tile_pool(name="cq", bufs=5))
-        gepool = ctx.enter_context(tc.tile_pool(name="ge", bufs=4))
-        gqpool = ctx.enter_context(tc.tile_pool(name="gq", bufs=3))
-        ccpool = ctx.enter_context(tc.tile_pool(name="cc", bufs=3))
-        opool = ctx.enter_context(tc.tile_pool(name="osb", bufs=3))
+        cqpool = ctx.enter_context(tc.tile_pool(name="cq", bufs=7))
+        gepool = ctx.enter_context(tc.tile_pool(name="ge", bufs=5))
+        gqpool = ctx.enter_context(tc.tile_pool(name="gq", bufs=4))
+        ccpool = ctx.enter_context(tc.tile_pool(name="cc", bufs=4))
+        opool = ctx.enter_context(tc.tile_pool(name="osb", bufs=6))
         psa = ctx.enter_context(tc.psum_pool(name="psa", bufs=2))
         psh = ctx.enter_context(tc.psum_pool(name="psh", bufs=6))
+        ctx.enter_context(tc.manual_schedule())
 
         x_codes = keep.tile([P, N_TOK], U32, align_bytes=64)
         x_scales = keep.tile([P, N_TOK], U8, align_bytes=64)
@@ -65,44 +73,29 @@ def tile_kan_t_kernel(tc, x, W, b, agg, out):
         warm = keep.tile([P, 2], F32)
 
         xr = {}
-
-        def load_x(g):
-            xraw = xpool.tile([P, TPC, D], BF16)
-            nc.sync.dma_start(out=xraw[:], in_=x_v[:, TPC * g:TPC * (g + 1), :])
-            xr[g] = xraw
-
-        load_x(0)
-        for u in range(2):
-            nc.scalar.dma_start(
-                out=w_raw[:, 2 * u:2 * u + 2, :],
-                in_=W[256 * u:256 * (u + 1), :].rearrange("(q e) c -> q e c", e=2),
-            )
-        nc.vector.memset(warm[:], 0.0)
-        nc.vector.memset(b_rows[:], 0.0)
-        for f in range(2):
-            for hf in range(2):
-                nc.gpsimd.dma_start(
-                    out=bms[f][H * hf:H * (hf + 1), :, :],
-                    in_=b[768 * f:768 * f + 256].rearrange("(p r h) -> p r h", r=2, h=2),
-                )
-        nc.scalar.activation(out=warm[:, 1:2], in_=warm[:, 0:1], func=ACT.Gelu)
-        for g in range(1, 5):
-            load_x(g)
-        make_identity(nc, ident_f[:])
-        nc.gpsimd.dma_start(out=b_rows[0:8, :], in_=b.rearrange("(m c) -> m c", c=P))
-        nc.gpsimd.dma_start(out=g_raw[0:H, 0, :, :], in_=agg[0:256, :].rearrange("(p t) o -> p t o", t=4))
-        nc.gpsimd.dma_start(out=g_raw[H:P, 0, :, :], in_=agg[768:1024, :].rearrange("(p t) o -> p t o", t=4))
-        nc.gpsimd.dma_start(out=g_raw[:, 1, :, :], in_=agg[256:768, :].rearrange("(t p) o -> p t o", p=P))
-        nc.vector.tensor_copy(out=bias_rg[0:H, 0, :], in_=bm_relu[0:H, :, 0])
-        nc.vector.tensor_copy(out=bias_rg[H:P, 0, :], in_=bm_relu[H:P, :, 1])
-        nc.vector.tensor_copy(out=bias_rg[0:H, 1, :], in_=bm_gelu[0:H, :, 1])
-        nc.vector.tensor_copy(out=bias_rg[H:P, 1, :], in_=bm_gelu[H:P, :, 0])
-
         xts = {}
         gxs = {}
+        hs = {}
+        cqs = {}
+        ges = {}
+        gqs = {}
+        ccs = {}
+        ops = {}
 
-        def transposes(g):
-            x32 = xr[g][:].rearrange("p i k -> p (i k)").bitcast(F32)
+        def load_x(c):
+            xraw = xpool.tile([P, TPC, D], BF16)
+            nc.sync.dma_start(out=xraw[:], in_=x_v[:, TPC * c:TPC * (c + 1), :])
+            xr[c] = xraw
+
+        def load_w(c0, c1):
+            for u in range(2):
+                nc.sync.dma_start(
+                    out=w_raw[:, 2 * u:2 * u + 2, c0:c1],
+                    in_=W[256 * u:256 * (u + 1), c0:c1].rearrange("(q e) c -> q e c", e=2),
+                )
+
+        def transposes(c):
+            x32 = xr[c][:].rearrange("p i k -> p (i k)").bitcast(F32)
             banks = []
             for a in range(2):
                 xt = psa.tile([P, 2, 2, P], F32, tag="a")
@@ -111,24 +104,24 @@ def tile_kan_t_kernel(tc, x, W, b, agg, out):
                         c0 = 256 * (2 * a + i2) + 128 * u
                         nc.tensor.transpose(xt[:, i2, u, :], x32[:, c0:c0 + P], ident_f[:])
                 banks.append(xt)
-            xts[g] = banks
+            xts[c] = banks
 
-        def x_evac(g):
+        def x_evac(c):
             gx = gxpool.tile([P, CH, 4], BF16, align_bytes=64)
-            gxs[g] = gx
+            gxs[c] = gx
             gx32 = gx[:].rearrange("p r t -> p (r t)").bitcast(F32).rearrange("p (r u) -> p r u", u=2)
             for a in range(2):
                 nc.scalar.copy(
                     out=gx32[:, 256 * a:256 * (a + 1), :].rearrange("p (i r) u -> p i r u", i=2),
-                    in_=xts[g][a][:].rearrange("p i u r -> p i r u"),
+                    in_=xts[c][a][:].rearrange("p i u r -> p i r u"),
                 )
 
-        def x_quant(g):
-            cols = slice(CH * g, CH * (g + 1))
+        def x_quant(c):
+            cols = slice(CH * c, CH * (c + 1))
             nc.vector.quantize_mx(
                 out=x_codes[:, cols].bitcast(FP8X4),
                 scales=x_scales[:, cols],
-                in_=gxs[g][:].rearrange("p r t -> p (r t)"),
+                in_=gxs[c][:].rearrange("p r t -> p (r t)"),
             )
 
         def w_regroup_relu():
@@ -157,98 +150,61 @@ def tile_kan_t_kernel(tc, x, W, b, agg, out):
                 in_=w_grp[:, cols, :].rearrange("p c t -> p (c t)"),
             )
 
-        def mx1(g, m):
-            h = psh.tile([P, CH], F32, tag="h")
-            nc.tensor.matmul_mx(
-                out=h[:],
-                lhsT=w_codes[:, P * m:P * (m + 1)].bitcast(FP8X4),
-                lhsT_scale=w_scales[:, P * m:P * (m + 1)],
-                rhs=x_codes[:, CH * g:CH * (g + 1)].bitcast(FP8X4),
-                rhs_scale=x_scales[:, CH * g:CH * (g + 1)],
-                start=True,
-                stop=True,
-            )
-            return h
+        def first_matmuls(tick):
+            c = tick % N_CH
+            m0 = 0 if tick < N_CH else 4
+            banks = []
+            for m in range(m0, m0 + 4):
+                h = psh.tile([P, CH], F32, tag="h")
+                nc.tensor.matmul_mx(
+                    out=h[:],
+                    lhsT=w_codes[:, P * m:P * (m + 1)].bitcast(FP8X4),
+                    lhsT_scale=w_scales[:, P * m:P * (m + 1)],
+                    rhs=x_codes[:, CH * c:CH * (c + 1)].bitcast(FP8X4),
+                    rhs_scale=x_scales[:, CH * c:CH * (c + 1)],
+                    start=True,
+                    stop=True,
+                )
+                banks.append(h)
+            hs[tick] = banks
 
-        def interleave(dst, src):
+        def relu(c, r):
+            on_vector = (c in V_RELU0) if r == 0 else (c not in S_RELU1)
+            if on_vector:
+                nc.vector.tensor_scalar(out=cqs[c][:, r, 0, :], in0=hs[c][r][:], scalar1=bias_rg[:, 0, r:r + 1],
+                                        scalar2=0.0, op0=ALU.add, op1=ALU.max)
+            else:
+                nc.scalar.activation(out=cqs[c][:, r, 0, :], in_=hs[c][r][:], func=ACT.Relu,
+                                     bias=bias_rg[:, 0, r:r + 1], scale=1.0)
+
+        def gelu(c, r):
+            nc.scalar.activation(out=ges[c][:, r, :], in_=hs[c][2 + r][:], func=ACT.Gelu,
+                                 bias=bias_rg[:, 1, r:r + 1], scale=1.0)
+
+        def tanh_sigmoid(c, t):
+            nc.scalar.activation(out=cqs[N_CH + c][:, t, :], in_=hs[N_CH + c][t][:],
+                                 func=(ACT.Tanh if t < 2 else ACT.Sigmoid),
+                                 bias=bias_ts[:, 2 + t:3 + t], scale=1.0)
+
+        def interleave(key, src):
+            gq = gqpool.tile([P, CH, 4], BF16, align_bytes=64)
+            gqs[key] = gq
             nc.vector.tensor_copy(
-                out=dst.rearrange("p (c i) t -> p c t i", i=4),
+                out=gq[:].rearrange("p (c i) t -> p c t i", i=4),
                 in_=src.rearrange("p t (c i) -> p c t i", i=4),
             )
 
-        def quant(codes, scales, grp):
+        def quant(codes, scales, key):
             nc.vector.quantize_mx(out=codes.bitcast(FP8X4), scales=scales,
-                                  in_=grp[:].rearrange("p r t -> p (r t)"))
+                                  in_=gqs[key][:].rearrange("p r t -> p (r t)"))
 
-        transposes(0)
-        x_evac(0)
-        w_regroup_relu()
-        w_regroup_gelu(0)
-        w_quant(0)
-        w_regroup_gelu(1)
-        x_quant(0)
-        w_quant(1)
-
-        for s in range(N_CH):
-            if s + 5 < N_CH:
-                load_x(s + 5)
-            if s + 1 < N_CH:
-                transposes(s + 1)
-                x_evac(s + 1)
-                x_quant(s + 1)
-            cq = cqpool.tile([P, 2, 2, CH], BF16, tag="cq")
-            ge = gepool.tile([P, 2, CH], BF16)
-            for r in range(2):
-                h = mx1(s, r)
-                if r == 0 or s % 2 == 1:
-                    nc.scalar.activation(out=cq[:, r, 0, :], in_=h[:], func=ACT.Relu,
-                                         bias=bias_rg[:, 0, r:r + 1], scale=1.0)
-                else:
-                    nc.vector.tensor_scalar(out=cq[:, r, 0, :], in0=h[:], scalar1=bias_rg[:, 0, r:r + 1],
-                                            scalar2=0.0, op0=ALU.add, op1=ALU.max)
-            nc.sync.dma_start(out=cq[0:H, :, 1, :], in_=cq[H:P, :, 0, :])
-            for r in range(2):
-                h = mx1(s, 2 + r)
-                nc.scalar.activation(out=ge[:, r, :], in_=h[:], func=ACT.Gelu,
-                                     bias=bias_rg[:, 1, r:r + 1], scale=1.0)
-            nc.sync.dma_start(out=cq[H:P, :, 1, :], in_=ge[0:H, :, :])
-            nc.sync.dma_start(out=cq[H:P, :, 0, :], in_=ge[H:P, :, :])
-            gq = gqpool.tile([P, CH, 4], BF16, align_bytes=64)
-            interleave(gq[:], cq[:].rearrange("p r h c -> p (r h) c"))
-            cols = slice(CH * s, CH * (s + 1))
-            quant(rg_codes[:, cols], rg_scales[:, cols], gq)
-            if s == 1:
-                nc.vector.tensor_copy(out=ident_b[:], in_=ident_f[:])
-                bt = psa.tile([P, P], BF16, tag="a")
-                nc.tensor.transpose(bt[:], b_rows[:], ident_b[:])
-                nc.vector.tensor_copy(out=bias_ts[:], in_=bt[:, 0:8])
-                w_regroup_ts(0)
-                w_regroup_ts(1)
-            if s == 2:
-                w_quant(2)
-                w_quant(3)
-                for q in range(2):
-                    nc.vector.tensor_copy(out=g_grp[:, q, :, :], in_=g_raw[:, q, :, :].rearrange("p t o -> p o t"))
-            if s == 3:
-                for q in range(2):
-                    nc.vector.quantize_mx(out=g_codes[:, q, :].bitcast(FP8X4), scales=g_scales[:, q, :],
-                                          in_=g_grp[:, q, :, :].rearrange("p o t -> p (o t)"))
-
-        for s in range(N_CH):
-            ct = cqpool.tile([P, 4, CH], BF16, tag="cq")
-            for t in range(4):
-                h = mx1(s, 4 + t)
-                nc.scalar.activation(out=ct[:, t, :], in_=h[:], func=(ACT.Tanh if t < 2 else ACT.Sigmoid),
-                                     bias=bias_ts[:, 2 + t:3 + t], scale=1.0)
-            gq = gqpool.tile([P, CH, 4], BF16, align_bytes=64)
-            interleave(gq[:], ct[:])
-            c_codes = ccpool.tile([P, CH], U32, align_bytes=64)
-            c_scales = ccpool.tile([P, CH], U8, align_bytes=64)
-            quant(c_codes[:], c_scales[:], gq)
+        def second_matmuls(c):
             o_ps = psa.tile([P, TPC, N_OUT], F32, tag="a")
+            ops[c] = o_ps
+            c_codes, c_scales = ccs[c]
             for j in range(TPC):
                 loc = slice(P * j, P * (j + 1))
-                glo = slice(CH * s + P * j, CH * s + P * (j + 1))
+                glo = slice(CH * c + P * j, CH * c + P * (j + 1))
                 pairs = ((rg_codes[:, glo], rg_scales[:, glo]), (c_codes[:, loc], c_scales[:, loc]))
                 for q, (cod, sca) in enumerate(pairs):
                     nc.tensor.matmul_mx(
@@ -260,6 +216,113 @@ def tile_kan_t_kernel(tc, x, W, b, agg, out):
                         start=(q == 0),
                         stop=(q == 1),
                     )
+
+        def store_out(c):
             o_sb = opool.tile([P, TPC, N_OUT], F32)
-            nc.vector.tensor_copy(out=o_sb[:], in_=o_ps[:])
-            nc.sync.dma_start(out=out_v[:, TPC * s:TPC * (s + 1), :], in_=o_sb[:])
+            if c in S_OUT:
+                nc.scalar.copy(out=o_sb[:], in_=ops[c][:])
+            else:
+                nc.vector.tensor_copy(out=o_sb[:], in_=ops[c][:])
+            nc.sync.dma_start(out=out_v[:, TPC * c:TPC * (c + 1), :], in_=o_sb[:])
+
+        for f in range(2):
+            for hf in range(2):
+                nc.scalar.dma_start(
+                    out=bms[f][H * hf:H * (hf + 1), :, :],
+                    in_=b[768 * f:768 * f + 256].rearrange("(p r h) -> p r h", r=2, h=2),
+                )
+        nc.vector.memset(b_rows[:], 0.0)
+        nc.vector.memset(warm[:], 0.0)
+        load_x(0)
+        load_w(0, 256)
+        load_x(1)
+        load_x(2)
+        load_w(768, 1024)
+        load_x(3)
+        load_w(256, 768)
+        load_x(4)
+        load_x(5)
+        nc.scalar.activation(out=warm[:, 1:2], in_=warm[:, 0:1], func=ACT.Gelu)
+        make_identity(nc, ident_f[:])
+        nc.gpsimd.dma_start(out=b_rows[0:8, :], in_=b.rearrange("(m c) -> m c", c=P))
+        nc.gpsimd.dma_start(out=g_raw[0:H, 0, :, :], in_=agg[0:256, :].rearrange("(p t) o -> p t o", t=4))
+        nc.gpsimd.dma_start(out=g_raw[H:P, 0, :, :], in_=agg[768:1024, :].rearrange("(p t) o -> p t o", t=4))
+        nc.gpsimd.dma_start(out=g_raw[:, 1, :, :], in_=agg[256:768, :].rearrange("(t p) o -> p t o", p=P))
+        nc.vector.tensor_copy(out=ident_b[:], in_=ident_f[:])
+        w_regroup_relu()
+        w_quant(0)
+
+        for tick in range(-4, 2 * N_CH + LAG_MM2 + 2):
+            c2 = tick - N_CH
+            if X_BUFS <= tick + 8 < N_CH:
+                load_x(tick + 8)
+            if 0 <= c2 - LAG_MM2 < N_CH:
+                second_matmuls(c2 - LAG_MM2)
+            if 0 <= tick < N_CH:
+                cqs[tick] = cqpool.tile([P, 2, 2, CH], BF16, tag="cq", name="cq")
+                relu(tick, 0)
+                relu(tick, 1)
+                nc.sync.dma_start(out=cqs[tick][0:H, :, 1, :], in_=cqs[tick][H:P, :, 0, :])
+            elif 0 <= c2 < N_CH:
+                cqs[tick] = cqpool.tile([P, 4, CH], BF16, tag="cq", name="ct")
+                tanh_sigmoid(c2, 0)
+                tanh_sigmoid(c2, 1)
+            if 0 <= tick + 1 < 2 * N_CH:
+                first_matmuls(tick + 1)
+            if 0 <= tick + 3 < N_CH:
+                x_evac(tick + 3)
+            if 0 <= tick < N_CH:
+                ges[tick] = gepool.tile([P, 2, CH], BF16, name="ge")
+                gelu(tick, 0)
+                gelu(tick, 1)
+                nc.sync.dma_start(out=cqs[tick][H:P, :, 1, :], in_=ges[tick][0:H, :, :])
+            elif 0 <= c2 < N_CH:
+                tanh_sigmoid(c2, 2)
+                tanh_sigmoid(c2, 3)
+            if 0 <= tick - 1 < N_CH:
+                nc.sync.dma_start(out=cqs[tick - 1][H:P, :, 0, :], in_=ges[tick - 1][H:P, :, :])
+            c1 = tick - LAG_MOVE
+            if 0 <= c1 < N_CH:
+                interleave(c1, cqs[c1][:].rearrange("p r h c -> p (r h) c"))
+            if tick == -1:
+                nc.vector.tensor_copy(out=bias_rg[0:H, 0, :], in_=bm_relu[0:H, :, 0])
+                nc.vector.tensor_copy(out=bias_rg[H:P, 0, :], in_=bm_relu[H:P, :, 1])
+                nc.vector.tensor_copy(out=bias_rg[0:H, 1, :], in_=bm_gelu[0:H, :, 1])
+                nc.vector.tensor_copy(out=bias_rg[H:P, 1, :], in_=bm_gelu[H:P, :, 0])
+            if 0 <= tick + 2 < N_CH:
+                x_quant(tick + 2)
+            if tick == -2:
+                w_regroup_gelu(0)
+                w_regroup_gelu(1)
+                w_quant(1)
+            if tick == 0:
+                w_regroup_ts(0)
+            if tick == 1:
+                w_regroup_ts(1)
+                w_quant(2)
+            if tick == 2:
+                w_quant(3)
+                for q in range(2):
+                    nc.vector.tensor_copy(out=g_grp[:, q, :, :], in_=g_raw[:, q, :, :].rearrange("p t o -> p o t"))
+            if 0 <= c1 - 1 < N_CH:
+                cols = slice(CH * (c1 - 1), CH * c1)
+                quant(rg_codes[:, cols], rg_scales[:, cols], c1 - 1)
+            if tick == 3:
+                for q in range(2):
+                    nc.vector.quantize_mx(out=g_codes[:, q, :].bitcast(FP8X4), scales=g_scales[:, q, :],
+                                          in_=g_grp[:, q, :, :].rearrange("p o t -> p (o t)"))
+            if 0 <= c2 - 1 < N_CH:
+                interleave(N_CH + c2 - 1, cqs[tick - 1][:])
+            if 0 <= c2 - 2 < N_CH:
+                c_codes = ccpool.tile([P, CH], U32, align_bytes=64)
+                c_scales = ccpool.tile([P, CH], U8, align_bytes=64)
+                ccs[c2 - 2] = (c_codes, c_scales)
+                quant(c_codes[:], c_scales[:], N_CH + c2 - 2)
+            if 0 <= c2 - LAG_MM2 - 1 < N_CH:
+                store_out(c2 - LAG_MM2 - 1)
+            if tick == 4:
+                bt = psa.tile([P, P], BF16, tag="a")
+                nc.tensor.transpose(bt[:], b_rows[:], ident_b[:])
+                nc.vector.tensor_copy(out=bias_ts[:], in_=bt[:, 0:8])
+            if 0 <= tick + 4 < N_CH:
+                transposes(tick + 4)

@@ -12,7 +12,6 @@ ACT = mybir.ActivationFunctionType
 ALU = mybir.AluOpType
 
 P = 128
-H = 64
 N_TOK = 8192
 D = 512
 N_BRANCH = 1024
@@ -30,6 +29,7 @@ LAG_MM2 = 4
 S_RELU1 = (13, 14, 15)
 V_RELU0 = (0, 1, 2)
 S_OUT = (11, 12, 13, 14)
+GELU_PIECES = ((0, 32, 0, 0), (32, 96, 0, 1), (96, 128, 32, 0))
 
 
 def tile_kan_t_kernel(tc, x, W, b, agg, out):
@@ -42,7 +42,7 @@ def tile_kan_t_kernel(tc, x, W, b, agg, out):
         xpool = ctx.enter_context(tc.tile_pool(name="xraw", bufs=X_BUFS))
         gxpool = ctx.enter_context(tc.tile_pool(name="gx", bufs=3))
         cqpool = ctx.enter_context(tc.tile_pool(name="cq", bufs=7))
-        gepool = ctx.enter_context(tc.tile_pool(name="ge", bufs=5))
+        repool = ctx.enter_context(tc.tile_pool(name="re", bufs=5))
         gqpool = ctx.enter_context(tc.tile_pool(name="gq", bufs=4))
         ccpool = ctx.enter_context(tc.tile_pool(name="cc", bufs=4))
         opool = ctx.enter_context(tc.tile_pool(name="osb", bufs=6))
@@ -66,10 +66,10 @@ def tile_kan_t_kernel(tc, x, W, b, agg, out):
         ident_b = keep.tile([P, P], BF16)
         b_rows = keep.tile([P, P], BF16)
         bias_ts = keep.tile([P, 8], F32)
-        bm_relu = keep.tile([P, 2, 2], BF16)
-        bm_gelu = keep.tile([P, 2, 2], BF16)
-        bms = (bm_relu, bm_gelu)
-        bias_rg = keep.tile([P, 2, 2], F32)
+        bm_relu = keep.tile([P, 2], BF16)
+        bm_gelu = keep.tile([P, 2], BF16)
+        bias_relu = keep.tile([P, 2], F32)
+        bias_gelu = keep.tile([P, 2], F32)
         warm = keep.tile([P, 2], F32)
 
         xr = {}
@@ -77,7 +77,7 @@ def tile_kan_t_kernel(tc, x, W, b, agg, out):
         gxs = {}
         hs = {}
         cqs = {}
-        ges = {}
+        res = {}
         gqs = {}
         ccs = {}
         ops = {}
@@ -126,14 +126,15 @@ def tile_kan_t_kernel(tc, x, W, b, agg, out):
 
         def w_regroup_relu():
             nc.vector.tensor_copy(
-                out=w_grp[:, 0:256, :].rearrange("p (t j) k -> p t j k", t=4),
-                in_=w_raw[:, :, 0:256].rearrange("p k (j t) -> p t j k", t=4),
+                out=w_grp[:, 0:256, :].rearrange("p (r m) k -> p r m k", r=2),
+                in_=w_raw[:, :, 0:256].rearrange("p k (m r) -> p r m k", r=2),
             )
 
-        def w_regroup_gelu(hf):
+        def w_regroup_gelu(piece):
+            m0, m1, j0, a = GELU_PIECES[piece]
             nc.vector.tensor_copy(
-                out=w_grp[:, 256:512, :].rearrange("p (r h j) k -> p r h j k", r=2, h=2)[:, :, hf, :, :],
-                in_=w_raw[:, :, 768:1024].rearrange("p k (j r g) -> p r g j k", r=2, g=2)[:, :, 1 - hf, :, :],
+                out=w_grp[:, 256:512, :].rearrange("p (r m) k -> p r m k", r=2)[:, :, m0:m1, :],
+                in_=w_raw[:, :, 768:1024].rearrange("p k (j a r) -> p r a j k", a=2, r=2)[:, :, a, j0:j0 + m1 - m0, :],
             )
 
         def w_regroup_ts(j):
@@ -171,15 +172,15 @@ def tile_kan_t_kernel(tc, x, W, b, agg, out):
         def relu(c, r):
             on_vector = (c in V_RELU0) if r == 0 else (c not in S_RELU1)
             if on_vector:
-                nc.vector.tensor_scalar(out=cqs[c][:, r, 0, :], in0=hs[c][r][:], scalar1=bias_rg[:, 0, r:r + 1],
+                nc.vector.tensor_scalar(out=res[c][:, r, :], in0=hs[c][r][:], scalar1=bias_relu[:, r:r + 1],
                                         scalar2=0.0, op0=ALU.add, op1=ALU.max)
             else:
-                nc.scalar.activation(out=cqs[c][:, r, 0, :], in_=hs[c][r][:], func=ACT.Relu,
-                                     bias=bias_rg[:, 0, r:r + 1], scale=1.0)
+                nc.scalar.activation(out=res[c][:, r, :], in_=hs[c][r][:], func=ACT.Relu,
+                                     bias=bias_relu[:, r:r + 1], scale=1.0)
 
         def gelu(c, r):
-            nc.scalar.activation(out=ges[c][:, r, :], in_=hs[c][2 + r][:], func=ACT.Gelu,
-                                 bias=bias_rg[:, 1, r:r + 1], scale=1.0)
+            nc.scalar.activation(out=cqs[c][:, r, :], in_=hs[c][2 + r][:], func=ACT.Gelu,
+                                 bias=bias_gelu[:, r:r + 1], scale=1.0)
 
         def tanh_sigmoid(c, t):
             nc.scalar.activation(out=cqs[N_CH + c][:, t, :], in_=hs[N_CH + c][t][:],
@@ -225,12 +226,12 @@ def tile_kan_t_kernel(tc, x, W, b, agg, out):
                 nc.vector.tensor_copy(out=o_sb[:], in_=ops[c][:])
             nc.sync.dma_start(out=out_v[:, TPC * c:TPC * (c + 1), :], in_=o_sb[:])
 
-        for f in range(2):
-            for hf in range(2):
-                nc.scalar.dma_start(
-                    out=bms[f][H * hf:H * (hf + 1), :, :],
-                    in_=b[768 * f:768 * f + 256].rearrange("(p r h) -> p r h", r=2, h=2),
-                )
+        nc.scalar.dma_start(out=bm_relu[:], in_=b[0:256].rearrange("(m r) -> m r", r=2))
+        for m0, m1, j0, a in GELU_PIECES:
+            nc.scalar.dma_start(
+                out=bm_gelu[m0:m1, :],
+                in_=b[768:1024].rearrange("(j a r) -> j a r", a=2, r=2)[j0:j0 + m1 - m0, a, :],
+            )
         nc.vector.memset(b_rows[:], 0.0)
         nc.vector.memset(warm[:], 0.0)
         load_x(0)
@@ -245,8 +246,9 @@ def tile_kan_t_kernel(tc, x, W, b, agg, out):
         nc.scalar.activation(out=warm[:, 1:2], in_=warm[:, 0:1], func=ACT.Gelu)
         make_identity(nc, ident_f[:])
         nc.gpsimd.dma_start(out=b_rows[0:8, :], in_=b.rearrange("(m c) -> m c", c=P))
-        nc.gpsimd.dma_start(out=g_raw[0:H, 0, :, :], in_=agg[0:256, :].rearrange("(p t) o -> p t o", t=4))
-        nc.gpsimd.dma_start(out=g_raw[H:P, 0, :, :], in_=agg[768:1024, :].rearrange("(p t) o -> p t o", t=4))
+        nc.gpsimd.dma_start(out=g_raw[32:96, 0, :, :], in_=agg[0:256, :].rearrange("(p t) o -> p t o", t=4))
+        nc.gpsimd.dma_start(out=g_raw[0:32, 0, :, :], in_=agg[768:896, :].rearrange("(p t) o -> p t o", t=4))
+        nc.gpsimd.dma_start(out=g_raw[96:128, 0, :, :], in_=agg[896:1024, :].rearrange("(p t) o -> p t o", t=4))
         nc.gpsimd.dma_start(out=g_raw[:, 1, :, :], in_=agg[256:768, :].rearrange("(t p) o -> p t o", p=P))
         nc.vector.tensor_copy(out=ident_b[:], in_=ident_f[:])
         w_regroup_relu()
@@ -259,10 +261,11 @@ def tile_kan_t_kernel(tc, x, W, b, agg, out):
             if 0 <= c2 - LAG_MM2 < N_CH:
                 second_matmuls(c2 - LAG_MM2)
             if 0 <= tick < N_CH:
-                cqs[tick] = cqpool.tile([P, 2, 2, CH], BF16, tag="cq", name="cq")
+                cqs[tick] = cqpool.tile([P, 4, CH], BF16, tag="cq", name="cq")
+                res[tick] = repool.tile([P, 2, CH], BF16, name="re")
                 relu(tick, 0)
                 relu(tick, 1)
-                nc.sync.dma_start(out=cqs[tick][0:H, :, 1, :], in_=cqs[tick][H:P, :, 0, :])
+                nc.sync.dma_start(out=cqs[tick][32:96, 2:4, :], in_=res[tick][1:P:2, :, :])
             elif 0 <= c2 < N_CH:
                 cqs[tick] = cqpool.tile([P, 4, CH], BF16, tag="cq", name="ct")
                 tanh_sigmoid(c2, 0)
@@ -272,28 +275,27 @@ def tile_kan_t_kernel(tc, x, W, b, agg, out):
             if 0 <= tick + 3 < N_CH:
                 x_evac(tick + 3)
             if 0 <= tick < N_CH:
-                ges[tick] = gepool.tile([P, 2, CH], BF16, name="ge")
                 gelu(tick, 0)
                 gelu(tick, 1)
-                nc.sync.dma_start(out=cqs[tick][H:P, :, 1, :], in_=ges[tick][0:H, :, :])
+                nc.sync.dma_start(out=cqs[tick][0:32, 2:4, :], in_=cqs[tick][32:64, 0:2, :])
+                nc.sync.dma_start(out=cqs[tick][96:128, 2:4, :], in_=cqs[tick][64:96, 0:2, :])
             elif 0 <= c2 < N_CH:
                 tanh_sigmoid(c2, 2)
                 tanh_sigmoid(c2, 3)
             if 0 <= tick - 1 < N_CH:
-                nc.sync.dma_start(out=cqs[tick - 1][H:P, :, 0, :], in_=ges[tick - 1][H:P, :, :])
+                nc.sync.dma_start(out=cqs[tick - 1][32:96, 0:2, :], in_=res[tick - 1][0:P:2, :, :])
             c1 = tick - LAG_MOVE
             if 0 <= c1 < N_CH:
-                interleave(c1, cqs[c1][:].rearrange("p r h c -> p (r h) c"))
+                interleave(c1, cqs[c1][:])
             if tick == -1:
-                nc.vector.tensor_copy(out=bias_rg[0:H, 0, :], in_=bm_relu[0:H, :, 0])
-                nc.vector.tensor_copy(out=bias_rg[H:P, 0, :], in_=bm_relu[H:P, :, 1])
-                nc.vector.tensor_copy(out=bias_rg[0:H, 1, :], in_=bm_gelu[0:H, :, 1])
-                nc.vector.tensor_copy(out=bias_rg[H:P, 1, :], in_=bm_gelu[H:P, :, 0])
+                nc.vector.tensor_copy(out=bias_relu[:], in_=bm_relu[:])
+                nc.vector.tensor_copy(out=bias_gelu[:], in_=bm_gelu[:])
             if 0 <= tick + 2 < N_CH:
                 x_quant(tick + 2)
             if tick == -2:
                 w_regroup_gelu(0)
                 w_regroup_gelu(1)
+                w_regroup_gelu(2)
                 w_quant(1)
             if tick == 0:
                 w_regroup_ts(0)

@@ -26,9 +26,12 @@ FLOPS = 2 * N_TOK * D * N_BRANCH + 2 * N_TOK * N_BRANCH * N_OUT
 X_BUFS = 6
 LAG_MOVE = 4
 LAG_MM2 = 4
-S_RELU1 = (13, 14, 15)
-V_RELU0 = (0, 1, 2)
-S_OUT = (11, 12, 13, 14)
+S_RELU1 = (14, 15)
+V_RELU0 = (0, 1, 2, 3)
+S_OUT = (10,)
+RAMP = -4
+LAST = N_CH - 1
+GELU_FIRST = (0,)
 GELU_PIECES = ((0, 32, 0, 0), (32, 96, 0, 1), (96, 128, 32, 0))
 
 
@@ -45,7 +48,7 @@ def tile_kan_t_kernel(tc, x, W, b, agg, out):
         repool = ctx.enter_context(tc.tile_pool(name="re", bufs=5))
         gqpool = ctx.enter_context(tc.tile_pool(name="gq", bufs=4))
         ccpool = ctx.enter_context(tc.tile_pool(name="cc", bufs=4))
-        opool = ctx.enter_context(tc.tile_pool(name="osb", bufs=6))
+        opool = ctx.enter_context(tc.tile_pool(name="osb", bufs=8))
         psa = ctx.enter_context(tc.psum_pool(name="psa", bufs=2))
         psh = ctx.enter_context(tc.psum_pool(name="psh", bufs=6))
         ctx.enter_context(tc.manual_schedule())
@@ -54,7 +57,9 @@ def tile_kan_t_kernel(tc, x, W, b, agg, out):
         x_scales = keep.tile([P, N_TOK], U8, align_bytes=64)
         rg_codes = keep.tile([P, N_TOK], U32, align_bytes=64)
         rg_scales = keep.tile([P, N_TOK], U8, align_bytes=64)
-        w_raw = keep.tile([P, 4, N_BRANCH], BF16)
+        w_raw_relu = keep.tile([P, 4, 256], BF16)
+        w_raw_gelu = keep.tile([P, 4, 256], BF16)
+        w_raw_ts = keep.tile([P, 4, 512], BF16)
         w_grp = keep.tile([P, N_BRANCH, 4], BF16, align_bytes=64)
         w_codes = keep.tile([P, N_BRANCH], U32, align_bytes=64)
         w_scales = keep.tile([P, N_BRANCH], U8, align_bytes=64)
@@ -87,10 +92,10 @@ def tile_kan_t_kernel(tc, x, W, b, agg, out):
             nc.sync.dma_start(out=xraw[:], in_=x_v[:, TPC * c:TPC * (c + 1), :])
             xr[c] = xraw
 
-        def load_w(c0, c1):
+        def load_w(w_raw, c0, c1):
             for u in range(2):
                 nc.sync.dma_start(
-                    out=w_raw[:, 2 * u:2 * u + 2, c0:c1],
+                    out=w_raw[:, 2 * u:2 * u + 2, :],
                     in_=W[256 * u:256 * (u + 1), c0:c1].rearrange("(q e) c -> q e c", e=2),
                 )
 
@@ -127,20 +132,20 @@ def tile_kan_t_kernel(tc, x, W, b, agg, out):
         def w_regroup_relu():
             nc.vector.tensor_copy(
                 out=w_grp[:, 0:256, :].rearrange("p (r m) k -> p r m k", r=2),
-                in_=w_raw[:, :, 0:256].rearrange("p k (m r) -> p r m k", r=2),
+                in_=w_raw_relu[:].rearrange("p k (m r) -> p r m k", r=2),
             )
 
         def w_regroup_gelu(piece):
             m0, m1, j0, a = GELU_PIECES[piece]
             nc.vector.tensor_copy(
                 out=w_grp[:, 256:512, :].rearrange("p (r m) k -> p r m k", r=2)[:, :, m0:m1, :],
-                in_=w_raw[:, :, 768:1024].rearrange("p k (j a r) -> p r a j k", a=2, r=2)[:, :, a, j0:j0 + m1 - m0, :],
+                in_=w_raw_gelu[:].rearrange("p k (j a r) -> p r a j k", a=2, r=2)[:, :, a, j0:j0 + m1 - m0, :],
             )
 
         def w_regroup_ts(j):
             nc.vector.tensor_copy(
                 out=w_grp[:, 256 * (j + 2):256 * (j + 3), :].rearrange("p (c i) t -> p c t i", i=4),
-                in_=w_raw[:, :, 256 * (j + 1):256 * (j + 2)].rearrange("p t (c i) -> p c t i", i=4),
+                in_=w_raw_ts[:, :, 256 * j:256 * (j + 1)].rearrange("p t (c i) -> p c t i", i=4),
             )
 
         def w_quant(j):
@@ -182,28 +187,39 @@ def tile_kan_t_kernel(tc, x, W, b, agg, out):
             nc.scalar.activation(out=cqs[c][:, r, :], in_=hs[c][2 + r][:], func=ACT.Gelu,
                                  bias=bias_gelu[:, r:r + 1], scale=1.0)
 
-        def tanh_sigmoid(c, t):
-            nc.scalar.activation(out=cqs[N_CH + c][:, t, :], in_=hs[N_CH + c][t][:],
+        def tanh_sigmoid(c, t, lo, hi):
+            nc.scalar.activation(out=cqs[N_CH + c][:, t, lo:hi], in_=hs[N_CH + c][t][:, lo:hi],
                                  func=(ACT.Tanh if t < 2 else ACT.Sigmoid),
                                  bias=bias_ts[:, 2 + t:3 + t], scale=1.0)
 
-        def interleave(key, src):
-            gq = gqpool.tile([P, CH, 4], BF16, align_bytes=64)
-            gqs[key] = gq
+        def interleave(key, src, lo, hi):
+            if lo == 0:
+                gq = gqpool.tile([P, CH, 4], BF16, align_bytes=64)
+                gqs[key] = gq
             nc.vector.tensor_copy(
-                out=gq[:].rearrange("p (c i) t -> p c t i", i=4),
-                in_=src.rearrange("p t (c i) -> p c t i", i=4),
+                out=gqs[key][:, lo:hi, :].rearrange("p (c i) t -> p c t i", i=4),
+                in_=src[:, :, lo:hi].rearrange("p t (c i) -> p c t i", i=4),
             )
 
-        def quant(codes, scales, key):
+        def quant(codes, scales, key, lo, hi):
             nc.vector.quantize_mx(out=codes.bitcast(FP8X4), scales=scales,
-                                  in_=gqs[key][:].rearrange("p r t -> p (r t)"))
+                                  in_=gqs[key][:, lo:hi, :].rearrange("p r t -> p (r t)"))
 
-        def second_matmuls(c):
-            o_ps = psa.tile([P, TPC, N_OUT], F32, tag="a")
-            ops[c] = o_ps
+        def quant_c2(c, lo, hi):
+            if lo == 0:
+                c_codes = ccpool.tile([P, CH], U32, align_bytes=64)
+                c_scales = ccpool.tile([P, CH], U8, align_bytes=64)
+                ccs[c] = (c_codes, c_scales)
+            quant(ccs[c][0][:, lo:hi], ccs[c][1][:, lo:hi], N_CH + c, lo, hi)
+
+        def second_matmuls(c, j0, j1):
+            if c < LAST - 3:
+                o_ps = psa.tile([P, TPC, N_OUT], F32, tag="a")
+            else:
+                o_ps = psh.tile([P, TPC, N_OUT], F32, tag="h")
+            ops[(c, j0)] = o_ps
             c_codes, c_scales = ccs[c]
-            for j in range(TPC):
+            for j in range(j0, j1):
                 loc = slice(P * j, P * (j + 1))
                 glo = slice(CH * c + P * j, CH * c + P * (j + 1))
                 pairs = ((rg_codes[:, glo], rg_scales[:, glo]), (c_codes[:, loc], c_scales[:, loc]))
@@ -218,13 +234,13 @@ def tile_kan_t_kernel(tc, x, W, b, agg, out):
                         stop=(q == 1),
                     )
 
-        def store_out(c):
+        def store_out(c, j0, j1, on_scalar):
             o_sb = opool.tile([P, TPC, N_OUT], F32)
-            if c in S_OUT:
-                nc.scalar.copy(out=o_sb[:], in_=ops[c][:])
+            if on_scalar:
+                nc.scalar.copy(out=o_sb[:, j0:j1, :], in_=ops[(c, j0)][:, j0:j1, :])
             else:
-                nc.vector.tensor_copy(out=o_sb[:], in_=ops[c][:])
-            nc.sync.dma_start(out=out_v[:, TPC * c:TPC * (c + 1), :], in_=o_sb[:])
+                nc.vector.tensor_copy(out=o_sb[:, j0:j1, :], in_=ops[(c, j0)][:, j0:j1, :])
+            nc.sync.dma_start(out=out_v[:, TPC * c + j0:TPC * c + j1, :], in_=o_sb[:, j0:j1, :])
 
         nc.scalar.dma_start(out=bm_relu[:], in_=b[0:256].rearrange("(m r) -> m r", r=2))
         for m0, m1, j0, a in GELU_PIECES:
@@ -232,99 +248,131 @@ def tile_kan_t_kernel(tc, x, W, b, agg, out):
                 out=bm_gelu[m0:m1, :],
                 in_=b[768:1024].rearrange("(j a r) -> j a r", a=2, r=2)[j0:j0 + m1 - m0, a, :],
             )
-        nc.vector.memset(b_rows[:], 0.0)
-        nc.vector.memset(warm[:], 0.0)
+        nc.gpsimd.memset(warm[:], 0.0)
         load_x(0)
-        load_w(0, 256)
+        load_w(w_raw_relu, 0, 256)
         load_x(1)
+        load_w(w_raw_gelu, 768, 1024)
         load_x(2)
-        load_w(768, 1024)
         load_x(3)
-        load_w(256, 768)
         load_x(4)
+        load_w(w_raw_ts, 256, 768)
         load_x(5)
         nc.scalar.activation(out=warm[:, 1:2], in_=warm[:, 0:1], func=ACT.Gelu)
         make_identity(nc, ident_f[:])
+        nc.gpsimd.memset(b_rows[:], 0.0)
         nc.gpsimd.dma_start(out=b_rows[0:8, :], in_=b.rearrange("(m c) -> m c", c=P))
         nc.gpsimd.dma_start(out=g_raw[32:96, 0, :, :], in_=agg[0:256, :].rearrange("(p t) o -> p t o", t=4))
         nc.gpsimd.dma_start(out=g_raw[0:32, 0, :, :], in_=agg[768:896, :].rearrange("(p t) o -> p t o", t=4))
         nc.gpsimd.dma_start(out=g_raw[96:128, 0, :, :], in_=agg[896:1024, :].rearrange("(p t) o -> p t o", t=4))
         nc.gpsimd.dma_start(out=g_raw[:, 1, :, :], in_=agg[256:768, :].rearrange("(t p) o -> p t o", p=P))
-        nc.vector.tensor_copy(out=ident_b[:], in_=ident_f[:])
+        transposes(0)
         w_regroup_relu()
         w_quant(0)
+        for piece in range(3):
+            w_regroup_gelu(piece)
 
-        for tick in range(-4, 2 * N_CH + LAG_MM2 + 2):
+        for tick in range(-3, 2 * N_CH):
             c2 = tick - N_CH
+            early = tick < RAMP
             if X_BUFS <= tick + 8 < N_CH:
                 load_x(tick + 8)
             if 0 <= c2 - LAG_MM2 < N_CH:
-                second_matmuls(c2 - LAG_MM2)
+                second_matmuls(c2 - LAG_MM2, 0, TPC)
             if 0 <= tick < N_CH:
                 cqs[tick] = cqpool.tile([P, 4, CH], BF16, tag="cq", name="cq")
                 res[tick] = repool.tile([P, 2, CH], BF16, name="re")
                 relu(tick, 0)
                 relu(tick, 1)
                 nc.sync.dma_start(out=cqs[tick][32:96, 2:4, :], in_=res[tick][1:P:2, :, :])
-            elif 0 <= c2 < N_CH:
+            elif c2 == LAST:
                 cqs[tick] = cqpool.tile([P, 4, CH], BF16, tag="cq", name="ct")
-                tanh_sigmoid(c2, 0)
-                tanh_sigmoid(c2, 1)
-            if 0 <= tick + 1 < 2 * N_CH:
+                for t in range(4):
+                    tanh_sigmoid(c2, t, 0, CH // 2)
+            elif 0 <= c2:
+                cqs[tick] = cqpool.tile([P, 4, CH], BF16, tag="cq", name="ct")
+                tanh_sigmoid(c2, 0, 0, CH)
+                tanh_sigmoid(c2, 1, 0, CH)
+            if -1 <= tick <= RAMP + 1:
+                x_quant(tick + 1)
+            if 0 < tick + 1 < 2 * N_CH:
                 first_matmuls(tick + 1)
-            if 0 <= tick + 3 < N_CH:
+            if tick == RAMP:
+                x_evac(tick + 2)
+                transposes(tick + 3)
+            if tick > RAMP and tick + 3 < N_CH and tick not in GELU_FIRST:
                 x_evac(tick + 3)
             if 0 <= tick < N_CH:
                 gelu(tick, 0)
                 gelu(tick, 1)
                 nc.sync.dma_start(out=cqs[tick][0:32, 2:4, :], in_=cqs[tick][32:64, 0:2, :])
                 nc.sync.dma_start(out=cqs[tick][96:128, 2:4, :], in_=cqs[tick][64:96, 0:2, :])
-            elif 0 <= c2 < N_CH:
-                tanh_sigmoid(c2, 2)
-                tanh_sigmoid(c2, 3)
+            elif c2 == LAST:
+                for t in range(4):
+                    tanh_sigmoid(c2, t, CH // 2, CH)
+            elif 0 <= c2:
+                tanh_sigmoid(c2, 2, 0, CH)
+                tanh_sigmoid(c2, 3, 0, CH)
+            if early:
+                x_evac(tick + 2)
+            if tick in GELU_FIRST:
+                x_evac(tick + 3)
+            if tick == RAMP:
+                x_evac(tick + 3)
             if 0 <= tick - 1 < N_CH:
                 nc.sync.dma_start(out=cqs[tick - 1][32:96, 0:2, :], in_=res[tick - 1][0:P:2, :, :])
             c1 = tick - LAG_MOVE
             if 0 <= c1 < N_CH:
-                interleave(c1, cqs[c1][:])
-            if tick == -1:
-                nc.vector.tensor_copy(out=bias_relu[:], in_=bm_relu[:])
-                nc.vector.tensor_copy(out=bias_gelu[:], in_=bm_gelu[:])
-            if 0 <= tick + 2 < N_CH:
+                interleave(c1, cqs[c1][:], 0, CH)
+            if RAMP + 1 <= tick and 0 <= tick + 2 < N_CH:
                 x_quant(tick + 2)
-            if tick == -2:
-                w_regroup_gelu(0)
-                w_regroup_gelu(1)
-                w_regroup_gelu(2)
-                w_quant(1)
-            if tick == 0:
+            if tick == 2:
                 w_regroup_ts(0)
-            if tick == 1:
+            if tick == 3:
                 w_regroup_ts(1)
                 w_quant(2)
-            if tick == 2:
+            if tick == 4:
                 w_quant(3)
                 for q in range(2):
                     nc.vector.tensor_copy(out=g_grp[:, q, :, :], in_=g_raw[:, q, :, :].rearrange("p t o -> p o t"))
             if 0 <= c1 - 1 < N_CH:
                 cols = slice(CH * (c1 - 1), CH * c1)
-                quant(rg_codes[:, cols], rg_scales[:, cols], c1 - 1)
-            if tick == 3:
+                quant(rg_codes[:, cols], rg_scales[:, cols], c1 - 1, 0, CH)
+            if tick == 5:
                 for q in range(2):
                     nc.vector.quantize_mx(out=g_codes[:, q, :].bitcast(FP8X4), scales=g_scales[:, q, :],
                                           in_=g_grp[:, q, :, :].rearrange("p o t -> p (o t)"))
-            if 0 <= c2 - 1 < N_CH:
-                interleave(N_CH + c2 - 1, cqs[tick - 1][:])
-            if 0 <= c2 - 2 < N_CH:
-                c_codes = ccpool.tile([P, CH], U32, align_bytes=64)
-                c_scales = ccpool.tile([P, CH], U8, align_bytes=64)
-                ccs[c2 - 2] = (c_codes, c_scales)
-                quant(c_codes[:], c_scales[:], N_CH + c2 - 2)
-            if 0 <= c2 - LAG_MM2 - 1 < N_CH:
-                store_out(c2 - LAG_MM2 - 1)
+            if 0 <= c2 - 1:
+                interleave(N_CH + c2 - 1, cqs[tick - 1][:], 0, CH)
+            if 0 <= c2 - 2:
+                quant_c2(c2 - 2, 0, CH)
+            if 0 <= c2 - LAG_MM2 - 1:
+                store_out(c2 - LAG_MM2 - 1, 0, TPC, c2 - LAG_MM2 - 1 in S_OUT)
             if tick == 4:
+                nc.vector.tensor_copy(out=ident_b[:], in_=ident_f[:])
                 bt = psa.tile([P, P], BF16, tag="a")
                 nc.tensor.transpose(bt[:], b_rows[:], ident_b[:])
                 nc.vector.tensor_copy(out=bias_ts[:], in_=bt[:, 0:8])
-            if 0 <= tick + 4 < N_CH:
-                transposes(tick + 4)
+            if tick == -2:
+                w_quant(1)
+                nc.vector.tensor_copy(out=bias_relu[:], in_=bm_relu[:])
+                nc.vector.tensor_copy(out=bias_gelu[:], in_=bm_gelu[:])
+                first_matmuls(0)
+            nxt = tick + 3 if early else tick + 4
+            if nxt < N_CH:
+                transposes(nxt)
+
+        interleave(N_CH + LAST, cqs[2 * N_CH - 1][:], 0, CH // 2)
+        second_matmuls(LAST - 3, 0, TPC)
+        second_matmuls(LAST - 2, 0, TPC)
+        quant_c2(LAST - 1, 0, CH)
+        interleave(N_CH + LAST, cqs[2 * N_CH - 1][:], CH // 2, CH)
+        quant_c2(LAST, 0, CH // 2)
+        quant_c2(LAST, CH // 2, CH)
+        second_matmuls(LAST - 1, 0, TPC)
+        second_matmuls(LAST, 0, TPC // 2)
+        second_matmuls(LAST, TPC // 2, TPC)
+        for c in range(LAST - 4, LAST):
+            store_out(c, 0, TPC, True)
+        store_out(LAST, 0, TPC // 2, True)
+        store_out(LAST, TPC // 2, TPC, False)

@@ -24,11 +24,11 @@ N_TT = N_TOK // P
 FLOPS = 2 * N_TOK * D * N_BRANCH + 2 * N_TOK * N_BRANCH * N_OUT
 
 X_BUFS = 6
-LAG_MOVE = 4
+LAG_MOVE = 5
 LAG_MM2 = 4
 S_RELU1 = (14, 15)
 V_RELU0 = (0, 1, 2, 3)
-S_OUT = (10,)
+S_OUT = (0, 1, 10)
 RAMP = -4
 LAST = N_CH - 1
 GELU_FIRST = (0,)
@@ -44,7 +44,7 @@ def tile_kan_t_kernel(tc, x, W, b, agg, out):
         keep = ctx.enter_context(tc.tile_pool(name="keep", bufs=1))
         xpool = ctx.enter_context(tc.tile_pool(name="xraw", bufs=X_BUFS))
         gxpool = ctx.enter_context(tc.tile_pool(name="gx", bufs=3))
-        cqpool = ctx.enter_context(tc.tile_pool(name="cq", bufs=7))
+        cqpool = ctx.enter_context(tc.tile_pool(name="cq", bufs=8))
         repool = ctx.enter_context(tc.tile_pool(name="re", bufs=5))
         gqpool = ctx.enter_context(tc.tile_pool(name="gq", bufs=4))
         ccpool = ctx.enter_context(tc.tile_pool(name="cc", bufs=4))
@@ -156,11 +156,11 @@ def tile_kan_t_kernel(tc, x, W, b, agg, out):
                 in_=w_grp[:, cols, :].rearrange("p c t -> p (c t)"),
             )
 
-        def first_matmuls(tick):
+        def first_matmuls(tick, lo=0, hi=4):
             c = tick % N_CH
             m0 = 0 if tick < N_CH else 4
-            banks = []
-            for m in range(m0, m0 + 4):
+            banks = hs.get(tick, [])
+            for m in range(m0 + lo, m0 + hi):
                 h = psh.tile([P, CH], F32, tag="h")
                 nc.tensor.matmul_mx(
                     out=h[:],
@@ -269,8 +269,6 @@ def tile_kan_t_kernel(tc, x, W, b, agg, out):
         transposes(0)
         w_regroup_relu()
         w_quant(0)
-        for piece in range(3):
-            w_regroup_gelu(piece)
 
         for tick in range(-3, 2 * N_CH):
             c2 = tick - N_CH
@@ -300,7 +298,7 @@ def tile_kan_t_kernel(tc, x, W, b, agg, out):
             if tick == RAMP:
                 x_evac(tick + 2)
                 transposes(tick + 3)
-            if tick > RAMP and tick + 3 < N_CH and tick not in GELU_FIRST:
+            if tick > RAMP and tick + 3 < N_CH and tick not in (-1, 0):
                 x_evac(tick + 3)
             if 0 <= tick < N_CH:
                 gelu(tick, 0)
@@ -315,8 +313,10 @@ def tile_kan_t_kernel(tc, x, W, b, agg, out):
                 tanh_sigmoid(c2, 3, 0, CH)
             if early:
                 x_evac(tick + 2)
-            if tick in GELU_FIRST:
-                x_evac(tick + 3)
+            if tick == 0:
+                x_evac(2)
+                transposes(3)
+                x_evac(3)
             if tick == RAMP:
                 x_evac(tick + 3)
             if 0 <= tick - 1 < N_CH:
@@ -354,12 +354,15 @@ def tile_kan_t_kernel(tc, x, W, b, agg, out):
                 nc.tensor.transpose(bt[:], b_rows[:], ident_b[:])
                 nc.vector.tensor_copy(out=bias_ts[:], in_=bt[:, 0:8])
             if tick == -2:
-                w_quant(1)
+                first_matmuls(0, 0, 2)
+                for piece in range(3):
+                    w_regroup_gelu(piece)
                 nc.vector.tensor_copy(out=bias_relu[:], in_=bm_relu[:])
+                w_quant(1)
                 nc.vector.tensor_copy(out=bias_gelu[:], in_=bm_gelu[:])
-                first_matmuls(0)
+                first_matmuls(0, 2, 4)
             nxt = tick + 3 if early else tick + 4
-            if nxt < N_CH:
+            if nxt < N_CH and tick != -1:
                 transposes(nxt)
 
         interleave(N_CH + LAST, cqs[2 * N_CH - 1][:], 0, CH // 2)

@@ -12,6 +12,7 @@ ACT = mybir.ActivationFunctionType
 ALU = mybir.AluOpType
 
 P = 128
+H = P // 2
 N_TOK = 8192
 D = 512
 N_BRANCH = 1024
@@ -24,15 +25,11 @@ N_TT = N_TOK // P
 FLOPS = 2 * N_TOK * D * N_BRANCH + 2 * N_TOK * N_BRANCH * N_OUT
 
 X_BUFS = 6
-LAG_MOVE = 5
+RELU_SCALE = 2.0 ** 40
 LAG_MM2 = 4
-S_RELU1 = (14, 15)
-V_RELU0 = (0, 1, 2, 3)
-S_OUT = (0, 1, 10)
-RAMP = -4
+S_EVAC = (0, 1)
+S_OUT = ()
 LAST = N_CH - 1
-GELU_FIRST = (0,)
-GELU_PIECES = ((0, 32, 0, 0), (32, 96, 0, 1), (96, 128, 32, 0))
 
 
 def tile_kan_t_kernel(tc, x, W, b, agg, out):
@@ -44,8 +41,7 @@ def tile_kan_t_kernel(tc, x, W, b, agg, out):
         keep = ctx.enter_context(tc.tile_pool(name="keep", bufs=1))
         xpool = ctx.enter_context(tc.tile_pool(name="xraw", bufs=X_BUFS))
         gxpool = ctx.enter_context(tc.tile_pool(name="gx", bufs=3))
-        cqpool = ctx.enter_context(tc.tile_pool(name="cq", bufs=8))
-        repool = ctx.enter_context(tc.tile_pool(name="re", bufs=5))
+        cqpool = ctx.enter_context(tc.tile_pool(name="cq", bufs=4))
         gqpool = ctx.enter_context(tc.tile_pool(name="gq", bufs=4))
         ccpool = ctx.enter_context(tc.tile_pool(name="cc", bufs=4))
         opool = ctx.enter_context(tc.tile_pool(name="osb", bufs=8))
@@ -68,13 +64,13 @@ def tile_kan_t_kernel(tc, x, W, b, agg, out):
         g_codes = keep.tile([P, 2, N_OUT], U32, align_bytes=64)
         g_scales = keep.tile([P, 2, N_OUT], U8, align_bytes=64)
         ident_f = keep.tile([P, P], F32)
-        ident_b = keep.tile([P, P], BF16)
-        b_rows = keep.tile([P, P], BF16)
-        bias_ts = keep.tile([P, 8], F32)
-        bm_relu = keep.tile([P, 2], BF16)
-        bm_gelu = keep.tile([P, 2], BF16)
-        bias_relu = keep.tile([P, 2], F32)
-        bias_gelu = keep.tile([P, 2], F32)
+        bm_rg = keep.tile([P, 4], BF16)
+        bm_tanh = keep.tile([P, 2], BF16)
+        bm_sig = keep.tile([P, 2], BF16)
+        bias_rg = keep.tile([P, 4], F32)
+        bias_ts = keep.tile([P, 4], F32)
+        lane_scale = keep.tile([P, 1], F32)
+        lane_unscale = keep.tile([P, 1], F32)
         warm = keep.tile([P, 2], F32)
 
         xr = {}
@@ -82,7 +78,6 @@ def tile_kan_t_kernel(tc, x, W, b, agg, out):
         gxs = {}
         hs = {}
         cqs = {}
-        res = {}
         gqs = {}
         ccs = {}
         ops = {}
@@ -111,15 +106,17 @@ def tile_kan_t_kernel(tc, x, W, b, agg, out):
                 banks.append(xt)
             xts[c] = banks
 
-        def x_evac(c):
-            gx = gxpool.tile([P, CH, 4], BF16, align_bytes=64)
-            gxs[c] = gx
-            gx32 = gx[:].rearrange("p r t -> p (r t)").bitcast(F32).rearrange("p (r u) -> p r u", u=2)
-            for a in range(2):
-                nc.scalar.copy(
-                    out=gx32[:, 256 * a:256 * (a + 1), :].rearrange("p (i r) u -> p i r u", i=2),
-                    in_=xts[c][a][:].rearrange("p i u r -> p i r u"),
-                )
+        def x_evac(c, a):
+            if a == 0:
+                gx = gxpool.tile([P, CH, 4], BF16, align_bytes=64)
+                gxs[c] = gx
+            gx32 = gxs[c][:].rearrange("p r t -> p (r t)").bitcast(F32).rearrange("p (r u) -> p r u", u=2)
+            dst = gx32[:, 256 * a:256 * (a + 1), :].rearrange("p (i r) u -> p i r u", i=2)
+            src = xts[c][a][:].rearrange("p i u r -> p i r u")
+            if a == 0 or c in S_EVAC:
+                nc.scalar.copy(out=dst, in_=src)
+            else:
+                nc.vector.tensor_copy(out=dst, in_=src)
 
         def x_quant(c):
             cols = slice(CH * c, CH * (c + 1))
@@ -129,23 +126,17 @@ def tile_kan_t_kernel(tc, x, W, b, agg, out):
                 in_=gxs[c][:].rearrange("p r t -> p (r t)"),
             )
 
-        def w_regroup_relu():
+        def w_regroup_rg(half):
+            w_raw = w_raw_gelu if half else w_raw_relu
             nc.vector.tensor_copy(
-                out=w_grp[:, 0:256, :].rearrange("p (r m) k -> p r m k", r=2),
-                in_=w_raw_relu[:].rearrange("p k (m r) -> p r m k", r=2),
+                out=w_grp[:, 0:512, :].rearrange("p (t h m) k -> p h t m k", t=4, h=2)[:, half, :, :, :],
+                in_=w_raw[:].rearrange("p k (m t) -> p t m k", t=4),
             )
 
-        def w_regroup_gelu(piece):
-            m0, m1, j0, a = GELU_PIECES[piece]
+        def w_regroup_ts(h):
             nc.vector.tensor_copy(
-                out=w_grp[:, 256:512, :].rearrange("p (r m) k -> p r m k", r=2)[:, :, m0:m1, :],
-                in_=w_raw_gelu[:].rearrange("p k (j a r) -> p r a j k", a=2, r=2)[:, :, a, j0:j0 + m1 - m0, :],
-            )
-
-        def w_regroup_ts(j):
-            nc.vector.tensor_copy(
-                out=w_grp[:, 256 * (j + 2):256 * (j + 3), :].rearrange("p (c i) t -> p c t i", i=4),
-                in_=w_raw_ts[:, :, 256 * j:256 * (j + 1)].rearrange("p t (c i) -> p c t i", i=4),
+                out=w_grp[:, 512 + 256 * h:768 + 256 * h, :].rearrange("p (e m) k -> p e m k", e=2),
+                in_=w_raw_ts[:, :, 256 * h:256 * (h + 1)].rearrange("p k (m e) -> p e m k", e=2),
             )
 
         def w_quant(j):
@@ -156,11 +147,11 @@ def tile_kan_t_kernel(tc, x, W, b, agg, out):
                 in_=w_grp[:, cols, :].rearrange("p c t -> p (c t)"),
             )
 
-        def first_matmuls(tick, lo=0, hi=4):
+        def first_matmuls(tick):
             c = tick % N_CH
             m0 = 0 if tick < N_CH else 4
-            banks = hs.get(tick, [])
-            for m in range(m0 + lo, m0 + hi):
+            banks = []
+            for m in range(m0, m0 + 4):
                 h = psh.tile([P, CH], F32, tag="h")
                 nc.tensor.matmul_mx(
                     out=h[:],
@@ -174,43 +165,37 @@ def tile_kan_t_kernel(tc, x, W, b, agg, out):
                 banks.append(h)
             hs[tick] = banks
 
-        def relu(c, r):
-            on_vector = (c in V_RELU0) if r == 0 else (c not in S_RELU1)
-            if on_vector:
-                nc.vector.tensor_scalar(out=res[c][:, r, :], in0=hs[c][r][:], scalar1=bias_relu[:, r:r + 1],
-                                        scalar2=0.0, op0=ALU.add, op1=ALU.max)
+        def activation(tick, t, lo=0, hi=CH):
+            dst = cqs[tick][:, t, lo:hi]
+            src = hs[tick][t][:, lo:hi]
+            if tick < N_CH:
+                nc.scalar.activation(out=dst, in_=src, func=ACT.Gelu, bias=bias_rg[:, t:t + 1], scale=lane_scale[:])
             else:
-                nc.scalar.activation(out=res[c][:, r, :], in_=hs[c][r][:], func=ACT.Relu,
-                                     bias=bias_relu[:, r:r + 1], scale=1.0)
+                nc.scalar.activation(out=dst, in_=src, func=(ACT.Tanh if t < 2 else ACT.Sigmoid),
+                                     bias=bias_ts[:, t:t + 1], scale=1.0)
 
-        def gelu(c, r):
-            nc.scalar.activation(out=cqs[c][:, r, :], in_=hs[c][2 + r][:], func=ACT.Gelu,
-                                 bias=bias_gelu[:, r:r + 1], scale=1.0)
-
-        def tanh_sigmoid(c, t, lo, hi):
-            nc.scalar.activation(out=cqs[N_CH + c][:, t, lo:hi], in_=hs[N_CH + c][t][:, lo:hi],
-                                 func=(ACT.Tanh if t < 2 else ACT.Sigmoid),
-                                 bias=bias_ts[:, 2 + t:3 + t], scale=1.0)
-
-        def interleave(key, src, lo, hi):
+        def interleave(tick, lo, hi):
             if lo == 0:
                 gq = gqpool.tile([P, CH, 4], BF16, align_bytes=64)
-                gqs[key] = gq
+                gqs[tick] = gq
             nc.vector.tensor_copy(
-                out=gqs[key][:, lo:hi, :].rearrange("p (c i) t -> p c t i", i=4),
-                in_=src[:, :, lo:hi].rearrange("p t (c i) -> p c t i", i=4),
+                out=gqs[tick][:, lo:hi, :].rearrange("p (c i) t -> p c t i", i=4),
+                in_=cqs[tick][:, :, lo:hi].rearrange("p t (c i) -> p c t i", i=4),
             )
 
-        def quant(codes, scales, key, lo, hi):
+        def quant(tick, lo, hi):
+            if tick < N_CH:
+                cols = slice(CH * tick + lo, CH * tick + hi)
+                codes, scales = rg_codes[:, cols], rg_scales[:, cols]
+            else:
+                if lo == 0:
+                    c_codes = ccpool.tile([P, CH], U32, align_bytes=64)
+                    c_scales = ccpool.tile([P, CH], U8, align_bytes=64)
+                    ccs[tick - N_CH] = (c_codes, c_scales)
+                c_codes, c_scales = ccs[tick - N_CH]
+                codes, scales = c_codes[:, lo:hi], c_scales[:, lo:hi]
             nc.vector.quantize_mx(out=codes.bitcast(FP8X4), scales=scales,
-                                  in_=gqs[key][:, lo:hi, :].rearrange("p r t -> p (r t)"))
-
-        def quant_c2(c, lo, hi):
-            if lo == 0:
-                c_codes = ccpool.tile([P, CH], U32, align_bytes=64)
-                c_scales = ccpool.tile([P, CH], U8, align_bytes=64)
-                ccs[c] = (c_codes, c_scales)
-            quant(ccs[c][0][:, lo:hi], ccs[c][1][:, lo:hi], N_CH + c, lo, hi)
+                                  in_=gqs[tick][:, lo:hi, :].rearrange("p r t -> p (r t)"))
 
         def second_matmuls(c, j0, j1):
             if c < LAST - 3:
@@ -242,90 +227,71 @@ def tile_kan_t_kernel(tc, x, W, b, agg, out):
                 nc.vector.tensor_copy(out=o_sb[:, j0:j1, :], in_=ops[(c, j0)][:, j0:j1, :])
             nc.sync.dma_start(out=out_v[:, TPC * c + j0:TPC * c + j1, :], in_=o_sb[:, j0:j1, :])
 
-        nc.scalar.dma_start(out=bm_relu[:], in_=b[0:256].rearrange("(m r) -> m r", r=2))
-        for m0, m1, j0, a in GELU_PIECES:
-            nc.scalar.dma_start(
-                out=bm_gelu[m0:m1, :],
-                in_=b[768:1024].rearrange("(j a r) -> j a r", a=2, r=2)[j0:j0 + m1 - m0, a, :],
-            )
+        nc.scalar.dma_start(out=bm_rg[0:H, :], in_=b[0:256].rearrange("(m t) -> m t", t=4))
+        nc.scalar.dma_start(out=bm_rg[H:P, :], in_=b[768:1024].rearrange("(m t) -> m t", t=4))
         nc.gpsimd.memset(warm[:], 0.0)
         load_x(0)
         load_w(w_raw_relu, 0, 256)
         load_x(1)
         load_w(w_raw_gelu, 768, 1024)
-        load_x(2)
-        load_x(3)
-        load_x(4)
+        for c in range(2, 5):
+            load_x(c)
         load_w(w_raw_ts, 256, 768)
         load_x(5)
         nc.scalar.activation(out=warm[:, 1:2], in_=warm[:, 0:1], func=ACT.Gelu)
         make_identity(nc, ident_f[:])
-        nc.gpsimd.memset(b_rows[:], 0.0)
-        nc.gpsimd.dma_start(out=b_rows[0:8, :], in_=b.rearrange("(m c) -> m c", c=P))
-        nc.gpsimd.dma_start(out=g_raw[32:96, 0, :, :], in_=agg[0:256, :].rearrange("(p t) o -> p t o", t=4))
-        nc.gpsimd.dma_start(out=g_raw[0:32, 0, :, :], in_=agg[768:896, :].rearrange("(p t) o -> p t o", t=4))
-        nc.gpsimd.dma_start(out=g_raw[96:128, 0, :, :], in_=agg[896:1024, :].rearrange("(p t) o -> p t o", t=4))
-        nc.gpsimd.dma_start(out=g_raw[:, 1, :, :], in_=agg[256:768, :].rearrange("(t p) o -> p t o", p=P))
+        nc.gpsimd.memset(lane_scale[0:H, :], RELU_SCALE)
+        nc.gpsimd.memset(lane_scale[H:P, :], 1.0)
+        nc.gpsimd.memset(lane_unscale[0:H, :], 1.0 / RELU_SCALE)
+        nc.gpsimd.memset(lane_unscale[H:P, :], 1.0)
+        nc.gpsimd.dma_start(out=bm_tanh[:], in_=b[256:512].rearrange("(p e) -> p e", e=2))
+        nc.gpsimd.dma_start(out=bm_sig[:], in_=b[512:768].rearrange("(p e) -> p e", e=2))
+        nc.gpsimd.dma_start(out=g_raw[0:H, 0, :, :], in_=agg[0:256, :].rearrange("(p t) o -> p t o", t=4))
+        nc.gpsimd.dma_start(out=g_raw[H:P, 0, :, :], in_=agg[768:1024, :].rearrange("(p t) o -> p t o", t=4))
+        for h in range(2):
+            nc.gpsimd.dma_start(
+                out=g_raw[:, 1, 2 * h:2 * h + 2, :],
+                in_=agg[256 + 256 * h:512 + 256 * h, :].rearrange("(p e) o -> p e o", e=2),
+            )
         transposes(0)
-        w_regroup_relu()
-        w_quant(0)
+        w_regroup_rg(0)
+        w_regroup_rg(1)
 
         for tick in range(-3, 2 * N_CH):
             c2 = tick - N_CH
-            early = tick < RAMP
             if X_BUFS <= tick + 8 < N_CH:
                 load_x(tick + 8)
-            if 0 <= c2 - LAG_MM2 < N_CH:
+            if 0 <= c2 - LAG_MM2:
                 second_matmuls(c2 - LAG_MM2, 0, TPC)
-            if 0 <= tick < N_CH:
-                cqs[tick] = cqpool.tile([P, 4, CH], BF16, tag="cq", name="cq")
-                res[tick] = repool.tile([P, 2, CH], BF16, name="re")
-                relu(tick, 0)
-                relu(tick, 1)
-                nc.sync.dma_start(out=cqs[tick][32:96, 2:4, :], in_=res[tick][1:P:2, :, :])
-            elif c2 == LAST:
-                cqs[tick] = cqpool.tile([P, 4, CH], BF16, tag="cq", name="ct")
-                for t in range(4):
-                    tanh_sigmoid(c2, t, 0, CH // 2)
-            elif 0 <= c2:
-                cqs[tick] = cqpool.tile([P, 4, CH], BF16, tag="cq", name="ct")
-                tanh_sigmoid(c2, 0, 0, CH)
-                tanh_sigmoid(c2, 1, 0, CH)
-            if -1 <= tick <= RAMP + 1:
-                x_quant(tick + 1)
-            if 0 < tick + 1 < 2 * N_CH:
+            if 0 <= tick:
+                cqs[tick] = cqpool.tile([P, 4, CH], BF16, name="cq")
+                if c2 == LAST:
+                    for t in range(4):
+                        activation(tick, t, 0, CH // 2)
+                else:
+                    activation(tick, 0)
+                    activation(tick, 1)
+            if -1 <= tick and tick + 1 < 2 * N_CH:
                 first_matmuls(tick + 1)
-            if tick == RAMP:
-                x_evac(tick + 2)
-                transposes(tick + 3)
-            if tick > RAMP and tick + 3 < N_CH and tick not in (-1, 0):
-                x_evac(tick + 3)
-            if 0 <= tick < N_CH:
-                gelu(tick, 0)
-                gelu(tick, 1)
-                nc.sync.dma_start(out=cqs[tick][0:32, 2:4, :], in_=cqs[tick][32:64, 0:2, :])
-                nc.sync.dma_start(out=cqs[tick][96:128, 2:4, :], in_=cqs[tick][64:96, 0:2, :])
-            elif c2 == LAST:
-                for t in range(4):
-                    tanh_sigmoid(c2, t, CH // 2, CH)
-            elif 0 <= c2:
-                tanh_sigmoid(c2, 2, 0, CH)
-                tanh_sigmoid(c2, 3, 0, CH)
-            if early:
-                x_evac(tick + 2)
-            if tick == 0:
-                x_evac(2)
-                transposes(3)
-                x_evac(3)
-            if tick == RAMP:
-                x_evac(tick + 3)
-            if 0 <= tick - 1 < N_CH:
-                nc.sync.dma_start(out=cqs[tick - 1][32:96, 0:2, :], in_=res[tick - 1][0:P:2, :, :])
-            c1 = tick - LAG_MOVE
-            if 0 <= c1 < N_CH:
-                interleave(c1, cqs[c1][:], 0, CH)
-            if RAMP + 1 <= tick and 0 <= tick + 2 < N_CH:
+            if tick + 3 < N_CH:
+                x_evac(tick + 3, 0)
+                x_evac(tick + 3, 1)
+            if 0 <= tick:
+                if c2 == LAST:
+                    for t in range(4):
+                        activation(tick, t, CH // 2, CH)
+                else:
+                    activation(tick, 2)
+                    activation(tick, 3)
+            if tick == -2:
+                w_quant(0)
+            if 0 <= tick + 2 < N_CH:
                 x_quant(tick + 2)
+            if tick == -2:
+                w_quant(1)
+                nc.vector.tensor_scalar(out=bias_rg[:], in0=bm_rg[:], scalar1=lane_scale[:, 0:1], scalar2=None, op0=ALU.mult)
+            if 0 <= tick - 2:
+                interleave(tick - 2, 0, CH)
             if tick == 2:
                 w_regroup_ts(0)
             if tick == 3:
@@ -333,45 +299,32 @@ def tile_kan_t_kernel(tc, x, W, b, agg, out):
                 w_quant(2)
             if tick == 4:
                 w_quant(3)
-                for q in range(2):
-                    nc.vector.tensor_copy(out=g_grp[:, q, :, :], in_=g_raw[:, q, :, :].rearrange("p t o -> p o t"))
-            if 0 <= c1 - 1 < N_CH:
-                cols = slice(CH * (c1 - 1), CH * c1)
-                quant(rg_codes[:, cols], rg_scales[:, cols], c1 - 1, 0, CH)
+                nc.vector.tensor_scalar(out=g_grp[:, 0, :, :], in0=g_raw[:, 0, :, :].rearrange("p t o -> p o t"),
+                                        scalar1=lane_unscale[:, 0:1], scalar2=None, op0=ALU.mult)
+                nc.vector.tensor_copy(out=g_grp[:, 1, :, :], in_=g_raw[:, 1, :, :].rearrange("p t o -> p o t"))
+                nc.vector.tensor_copy(out=bias_ts[:, 0:2], in_=bm_tanh[:])
+                nc.vector.tensor_copy(out=bias_ts[:, 2:4], in_=bm_sig[:])
+            if 0 <= tick - 3:
+                quant(tick - 3, 0, CH)
             if tick == 5:
                 for q in range(2):
                     nc.vector.quantize_mx(out=g_codes[:, q, :].bitcast(FP8X4), scales=g_scales[:, q, :],
                                           in_=g_grp[:, q, :, :].rearrange("p o t -> p (o t)"))
-            if 0 <= c2 - 1:
-                interleave(N_CH + c2 - 1, cqs[tick - 1][:], 0, CH)
-            if 0 <= c2 - 2:
-                quant_c2(c2 - 2, 0, CH)
             if 0 <= c2 - LAG_MM2 - 1:
                 store_out(c2 - LAG_MM2 - 1, 0, TPC, c2 - LAG_MM2 - 1 in S_OUT)
-            if tick == 4:
-                nc.vector.tensor_copy(out=ident_b[:], in_=ident_f[:])
-                bt = psa.tile([P, P], BF16, tag="a")
-                nc.tensor.transpose(bt[:], b_rows[:], ident_b[:])
-                nc.vector.tensor_copy(out=bias_ts[:], in_=bt[:, 0:8])
-            if tick == -2:
-                first_matmuls(0, 0, 2)
-                for piece in range(3):
-                    w_regroup_gelu(piece)
-                nc.vector.tensor_copy(out=bias_relu[:], in_=bm_relu[:])
-                w_quant(1)
-                nc.vector.tensor_copy(out=bias_gelu[:], in_=bm_gelu[:])
-                first_matmuls(0, 2, 4)
-            nxt = tick + 3 if early else tick + 4
-            if nxt < N_CH and tick != -1:
-                transposes(nxt)
+            if tick + 4 < N_CH:
+                transposes(tick + 4)
 
-        interleave(N_CH + LAST, cqs[2 * N_CH - 1][:], 0, CH // 2)
+        end = 2 * N_CH - 1
+        interleave(end - 1, 0, CH)
+        quant(end - 2, 0, CH)
+        interleave(end, 0, CH // 2)
         second_matmuls(LAST - 3, 0, TPC)
         second_matmuls(LAST - 2, 0, TPC)
-        quant_c2(LAST - 1, 0, CH)
-        interleave(N_CH + LAST, cqs[2 * N_CH - 1][:], CH // 2, CH)
-        quant_c2(LAST, 0, CH // 2)
-        quant_c2(LAST, CH // 2, CH)
+        quant(end - 1, 0, CH)
+        interleave(end, CH // 2, CH)
+        quant(end, 0, CH // 2)
+        quant(end, CH // 2, CH)
         second_matmuls(LAST - 1, 0, TPC)
         second_matmuls(LAST, 0, TPC // 2)
         second_matmuls(LAST, TPC // 2, TPC)

@@ -28,8 +28,12 @@ X_BUFS = 6
 RELU_SCALE = 2.0 ** 40
 LAG_MM2 = 4
 S_EVAC = (0, 1)
+V_EVAC = (4, 10)
 S_OUT = ()
 LAST = N_CH - 1
+G_TOK = 0
+V_SKIP = (7,)
+V_TWO = (18,)
 
 
 def tile_kan_t_kernel(tc, x, W, b, agg, out):
@@ -41,7 +45,7 @@ def tile_kan_t_kernel(tc, x, W, b, agg, out):
         keep = ctx.enter_context(tc.tile_pool(name="keep", bufs=1))
         xpool = ctx.enter_context(tc.tile_pool(name="xraw", bufs=X_BUFS))
         gxpool = ctx.enter_context(tc.tile_pool(name="gx", bufs=3))
-        cqpool = ctx.enter_context(tc.tile_pool(name="cq", bufs=4))
+        cqpool = ctx.enter_context(tc.tile_pool(name="cq", bufs=6))
         gqpool = ctx.enter_context(tc.tile_pool(name="gq", bufs=4))
         ccpool = ctx.enter_context(tc.tile_pool(name="cc", bufs=4))
         opool = ctx.enter_context(tc.tile_pool(name="osb", bufs=8))
@@ -84,8 +88,10 @@ def tile_kan_t_kernel(tc, x, W, b, agg, out):
 
         def load_x(c):
             xraw = xpool.tile([P, TPC, D], BF16)
-            nc.sync.dma_start(out=xraw[:], in_=x_v[:, TPC * c:TPC * (c + 1), :])
             xr[c] = xraw
+            n = 2 if c == 0 else TPC
+            for i in range(0, TPC, n):
+                nc.sync.dma_start(out=xraw[:, i:i + n, :], in_=x_v[:, TPC * c + i:TPC * c + i + n, :])
 
         def load_w(w_raw, c0, c1):
             for u in range(2):
@@ -113,7 +119,7 @@ def tile_kan_t_kernel(tc, x, W, b, agg, out):
             gx32 = gxs[c][:].rearrange("p r t -> p (r t)").bitcast(F32).rearrange("p (r u) -> p r u", u=2)
             dst = gx32[:, 256 * a:256 * (a + 1), :].rearrange("p (i r) u -> p i r u", i=2)
             src = xts[c][a][:].rearrange("p i u r -> p i r u")
-            if a == 0 or c in S_EVAC:
+            if c in S_EVAC or (a == 0 and c not in V_EVAC):
                 nc.scalar.copy(out=dst, in_=src)
             else:
                 nc.vector.tensor_copy(out=dst, in_=src)
@@ -234,10 +240,11 @@ def tile_kan_t_kernel(tc, x, W, b, agg, out):
         load_w(w_raw_relu, 0, 256)
         load_x(1)
         load_w(w_raw_gelu, 768, 1024)
-        for c in range(2, 5):
-            load_x(c)
+        load_x(2)
+        load_x(3)
         load_w(w_raw_ts, 256, 768)
-        load_x(5)
+        for c in range(4, X_BUFS):
+            load_x(c)
         nc.scalar.activation(out=warm[:, 1:2], in_=warm[:, 0:1], func=ACT.Gelu)
         make_identity(nc, ident_f[:])
         nc.gpsimd.memset(lane_scale[0:H, :], RELU_SCALE)
@@ -257,6 +264,8 @@ def tile_kan_t_kernel(tc, x, W, b, agg, out):
         w_regroup_rg(0)
         w_regroup_rg(1)
 
+        todo = 0
+        quantised = 0
         for tick in range(-3, 2 * N_CH):
             c2 = tick - N_CH
             if X_BUFS <= tick + 8 < N_CH:
@@ -283,35 +292,43 @@ def tile_kan_t_kernel(tc, x, W, b, agg, out):
                 else:
                     activation(tick, 2)
                     activation(tick, 3)
+            if 0 <= c2 - LAG_MM2 - 1:
+                store_out(c2 - LAG_MM2 - 1, 0, TPC, c2 - LAG_MM2 - 1 in S_OUT)
             if tick == -2:
                 w_quant(0)
-            if 0 <= tick + 2 < N_CH:
+            if 0 <= tick + 2 < N_CH and tick < 2:
                 x_quant(tick + 2)
             if tick == -2:
                 w_quant(1)
                 nc.vector.tensor_scalar(out=bias_rg[:], in0=bm_rg[:], scalar1=lane_scale[:, 0:1], scalar2=None, op0=ALU.mult)
-            if 0 <= tick - 2:
-                interleave(tick - 2, 0, CH)
-            if tick == 2:
+            for k in range(0 if tick < 2 or tick in V_SKIP else 2 if tick in V_TWO else 1):
+                interleave(todo, 0, CH)
+                if k == 1:
+                    quant(quantised, 0, CH)
+                    quantised += 1
+                todo += 1
+            if tick == 0:
                 w_regroup_ts(0)
-            if tick == 3:
+            if tick == 1:
                 w_regroup_ts(1)
                 w_quant(2)
-            if tick == 4:
+            if tick == 2:
                 w_quant(3)
+            if tick == 1:
                 nc.vector.tensor_scalar(out=g_grp[:, 0, :, :], in0=g_raw[:, 0, :, :].rearrange("p t o -> p o t"),
                                         scalar1=lane_unscale[:, 0:1], scalar2=None, op0=ALU.mult)
                 nc.vector.tensor_copy(out=g_grp[:, 1, :, :], in_=g_raw[:, 1, :, :].rearrange("p t o -> p o t"))
                 nc.vector.tensor_copy(out=bias_ts[:, 0:2], in_=bm_tanh[:])
                 nc.vector.tensor_copy(out=bias_ts[:, 2:4], in_=bm_sig[:])
-            if 0 <= tick - 3:
-                quant(tick - 3, 0, CH)
-            if tick == 5:
+            if 2 <= tick and tick + 2 < N_CH:
+                x_quant(tick + 2)
+            if quantised < todo - 1:
+                quant(quantised, 0, CH)
+                quantised += 1
+            if tick == 2:
                 for q in range(2):
                     nc.vector.quantize_mx(out=g_codes[:, q, :].bitcast(FP8X4), scales=g_scales[:, q, :],
                                           in_=g_grp[:, q, :, :].rearrange("p o t -> p (o t)"))
-            if 0 <= c2 - LAG_MM2 - 1:
-                store_out(c2 - LAG_MM2 - 1, 0, TPC, c2 - LAG_MM2 - 1 in S_OUT)
             if tick + 4 < N_CH:
                 transposes(tick + 4)
 

@@ -28,12 +28,12 @@ X_BUFS = 6
 RELU_SCALE = 2.0 ** 40
 LAG_MM2 = 4
 S_EVAC = (0, 1)
-V_EVAC = (4, 10)
+V_EVAC = ()
 S_OUT = ()
 LAST = N_CH - 1
 G_TOK = 0
-V_SKIP = (7,)
-V_TWO = (18,)
+V_SKIP = ()
+V_TWO = ()
 
 
 def tile_kan_t_kernel(tc, x, W, b, agg, out):
@@ -45,7 +45,7 @@ def tile_kan_t_kernel(tc, x, W, b, agg, out):
         keep = ctx.enter_context(tc.tile_pool(name="keep", bufs=1))
         xpool = ctx.enter_context(tc.tile_pool(name="xraw", bufs=X_BUFS))
         gxpool = ctx.enter_context(tc.tile_pool(name="gx", bufs=3))
-        cqpool = ctx.enter_context(tc.tile_pool(name="cq", bufs=6))
+        cqpool = ctx.enter_context(tc.tile_pool(name="cq", bufs=4))
         gqpool = ctx.enter_context(tc.tile_pool(name="gq", bufs=4))
         ccpool = ctx.enter_context(tc.tile_pool(name="cc", bufs=4))
         opool = ctx.enter_context(tc.tile_pool(name="osb", bufs=8))
@@ -59,7 +59,8 @@ def tile_kan_t_kernel(tc, x, W, b, agg, out):
         rg_scales = keep.tile([P, N_TOK], U8, align_bytes=64)
         w_raw_relu = keep.tile([P, 4, 256], BF16)
         w_raw_gelu = keep.tile([P, 4, 256], BF16)
-        w_raw_ts = keep.tile([P, 4, 512], BF16)
+        w_raw_tanh = keep.tile([P, 4, 256], BF16)
+        w_raw_sig = keep.tile([P, 4, 256], BF16)
         w_grp = keep.tile([P, N_BRANCH, 4], BF16, align_bytes=64)
         w_codes = keep.tile([P, N_BRANCH], U32, align_bytes=64)
         w_scales = keep.tile([P, N_BRANCH], U8, align_bytes=64)
@@ -69,12 +70,13 @@ def tile_kan_t_kernel(tc, x, W, b, agg, out):
         g_scales = keep.tile([P, 2, N_OUT], U8, align_bytes=64)
         ident_f = keep.tile([P, P], F32)
         bm_rg = keep.tile([P, 4], BF16)
-        bm_tanh = keep.tile([P, 2], BF16)
-        bm_sig = keep.tile([P, 2], BF16)
+        bm_ts = keep.tile([P, 4], BF16)
         bias_rg = keep.tile([P, 4], F32)
         bias_ts = keep.tile([P, 4], F32)
         lane_scale = keep.tile([P, 1], F32)
         lane_unscale = keep.tile([P, 1], F32)
+        lane_half = keep.tile([P, 1], F32)
+        lane_add = keep.tile([P, 1], F32)
         warm = keep.tile([P, 2], F32)
 
         xr = {}
@@ -132,18 +134,20 @@ def tile_kan_t_kernel(tc, x, W, b, agg, out):
                 in_=gxs[c][:].rearrange("p r t -> p (r t)"),
             )
 
-        def w_regroup_rg(half):
-            w_raw = w_raw_gelu if half else w_raw_relu
-            nc.vector.tensor_copy(
-                out=w_grp[:, 0:512, :].rearrange("p (t h m) k -> p h t m k", t=4, h=2)[:, half, :, :, :],
-                in_=w_raw[:].rearrange("p k (m t) -> p t m k", t=4),
+        def w_regroup(w_raw, c0, half, factor):
+            nc.vector.tensor_scalar(
+                out=w_grp[:, c0:c0 + 512, :].rearrange("p (t h m) k -> p h t m k", t=4, h=2)[:, half, :, :, :],
+                in0=w_raw[:].rearrange("p k (m t) -> p t m k", t=4),
+                scalar1=factor,
+                scalar2=None,
+                op0=ALU.mult,
             )
 
-        def w_regroup_ts(h):
-            nc.vector.tensor_copy(
-                out=w_grp[:, 512 + 256 * h:768 + 256 * h, :].rearrange("p (e m) k -> p e m k", e=2),
-                in_=w_raw_ts[:, :, 256 * h:256 * (h + 1)].rearrange("p k (m e) -> p e m k", e=2),
-            )
+        def w_regroup_rg(half):
+            w_regroup(w_raw_gelu if half else w_raw_relu, 0, half, 1.0 if half else RELU_SCALE)
+
+        def w_regroup_ts(half):
+            w_regroup(w_raw_sig if half else w_raw_tanh, 512, half, 0.5 if half else 1.0)
 
         def w_quant(j):
             cols = slice(256 * j, 256 * (j + 1))
@@ -175,19 +179,20 @@ def tile_kan_t_kernel(tc, x, W, b, agg, out):
             dst = cqs[tick][:, t, lo:hi]
             src = hs[tick][t][:, lo:hi]
             if tick < N_CH:
-                nc.scalar.activation(out=dst, in_=src, func=ACT.Gelu, bias=bias_rg[:, t:t + 1], scale=lane_scale[:])
+                nc.scalar.activation(out=dst, in_=src, func=ACT.Gelu, bias=bias_rg[:, t:t + 1], scale=1.0)
             else:
-                nc.scalar.activation(out=dst, in_=src, func=(ACT.Tanh if t < 2 else ACT.Sigmoid),
-                                     bias=bias_ts[:, t:t + 1], scale=1.0)
+                nc.scalar.activation(out=dst, in_=src, func=ACT.Tanh, bias=bias_ts[:, t:t + 1], scale=1.0)
 
         def interleave(tick, lo, hi):
             if lo == 0:
                 gq = gqpool.tile([P, CH, 4], BF16, align_bytes=64)
                 gqs[tick] = gq
-            nc.vector.tensor_copy(
-                out=gqs[tick][:, lo:hi, :].rearrange("p (c i) t -> p c t i", i=4),
-                in_=cqs[tick][:, :, lo:hi].rearrange("p t (c i) -> p c t i", i=4),
-            )
+            dst = gqs[tick][:, lo:hi, :].rearrange("p (c i) t -> p c t i", i=4)
+            src = cqs[tick][:, :, lo:hi].rearrange("p t (c i) -> p c t i", i=4)
+            if tick < N_CH:
+                nc.vector.tensor_copy(out=dst, in_=src)
+            else:
+                nc.vector.tensor_scalar(out=dst, in0=src, scalar1=lane_add[:], scalar2=None, op0=ALU.add)
 
         def quant(tick, lo, hi):
             if tick < N_CH:
@@ -242,7 +247,8 @@ def tile_kan_t_kernel(tc, x, W, b, agg, out):
         load_w(w_raw_gelu, 768, 1024)
         load_x(2)
         load_x(3)
-        load_w(w_raw_ts, 256, 768)
+        load_w(w_raw_tanh, 256, 512)
+        load_w(w_raw_sig, 512, 768)
         for c in range(4, X_BUFS):
             load_x(c)
         nc.scalar.activation(out=warm[:, 1:2], in_=warm[:, 0:1], func=ACT.Gelu)
@@ -251,18 +257,18 @@ def tile_kan_t_kernel(tc, x, W, b, agg, out):
         nc.gpsimd.memset(lane_scale[H:P, :], 1.0)
         nc.gpsimd.memset(lane_unscale[0:H, :], 1.0 / RELU_SCALE)
         nc.gpsimd.memset(lane_unscale[H:P, :], 1.0)
-        nc.gpsimd.dma_start(out=bm_tanh[:], in_=b[256:512].rearrange("(p e) -> p e", e=2))
-        nc.gpsimd.dma_start(out=bm_sig[:], in_=b[512:768].rearrange("(p e) -> p e", e=2))
+        nc.gpsimd.memset(lane_half[0:H, :], 1.0)
+        nc.gpsimd.memset(lane_half[H:P, :], 0.5)
+        nc.gpsimd.memset(lane_add[0:H, :], 0.0)
+        nc.gpsimd.memset(lane_add[H:P, :], 1.0)
+        nc.gpsimd.dma_start(out=bm_ts[0:H, :], in_=b[256:512].rearrange("(m t) -> m t", t=4))
+        nc.gpsimd.dma_start(out=bm_ts[H:P, :], in_=b[512:768].rearrange("(m t) -> m t", t=4))
         nc.gpsimd.dma_start(out=g_raw[0:H, 0, :, :], in_=agg[0:256, :].rearrange("(p t) o -> p t o", t=4))
         nc.gpsimd.dma_start(out=g_raw[H:P, 0, :, :], in_=agg[768:1024, :].rearrange("(p t) o -> p t o", t=4))
-        for h in range(2):
-            nc.gpsimd.dma_start(
-                out=g_raw[:, 1, 2 * h:2 * h + 2, :],
-                in_=agg[256 + 256 * h:512 + 256 * h, :].rearrange("(p e) o -> p e o", e=2),
-            )
+        nc.gpsimd.dma_start(out=g_raw[0:H, 1, :, :], in_=agg[256:512, :].rearrange("(p t) o -> p t o", t=4))
+        nc.gpsimd.dma_start(out=g_raw[H:P, 1, :, :], in_=agg[512:768, :].rearrange("(p t) o -> p t o", t=4))
         transposes(0)
         w_regroup_rg(0)
-        w_regroup_rg(1)
 
         todo = 0
         quantised = 0
@@ -273,7 +279,7 @@ def tile_kan_t_kernel(tc, x, W, b, agg, out):
             if 0 <= c2 - LAG_MM2:
                 second_matmuls(c2 - LAG_MM2, 0, TPC)
             if 0 <= tick:
-                cqs[tick] = cqpool.tile([P, 4, CH], BF16, name="cq")
+                cqs[tick] = cqpool.tile([P, 4, CH], BF16 if tick < N_CH else F32, tag=("cq" if tick < N_CH else "ct"), name="cq")
                 if c2 == LAST:
                     for t in range(4):
                         activation(tick, t, 0, CH // 2)
@@ -294,11 +300,11 @@ def tile_kan_t_kernel(tc, x, W, b, agg, out):
                     activation(tick, 3)
             if 0 <= c2 - LAG_MM2 - 1:
                 store_out(c2 - LAG_MM2 - 1, 0, TPC, c2 - LAG_MM2 - 1 in S_OUT)
-            if tick == -2:
-                w_quant(0)
-            if 0 <= tick + 2 < N_CH and tick < 2:
+            if 0 <= tick + 2 < N_CH:
                 x_quant(tick + 2)
             if tick == -2:
+                w_regroup_rg(1)
+                w_quant(0)
                 w_quant(1)
                 nc.vector.tensor_scalar(out=bias_rg[:], in0=bm_rg[:], scalar1=lane_scale[:, 0:1], scalar2=None, op0=ALU.mult)
             for k in range(0 if tick < 2 or tick in V_SKIP else 2 if tick in V_TWO else 1):
@@ -315,13 +321,10 @@ def tile_kan_t_kernel(tc, x, W, b, agg, out):
             if tick == 2:
                 w_quant(3)
             if tick == 1:
-                nc.vector.tensor_scalar(out=g_grp[:, 0, :, :], in0=g_raw[:, 0, :, :].rearrange("p t o -> p o t"),
-                                        scalar1=lane_unscale[:, 0:1], scalar2=None, op0=ALU.mult)
-                nc.vector.tensor_copy(out=g_grp[:, 1, :, :], in_=g_raw[:, 1, :, :].rearrange("p t o -> p o t"))
-                nc.vector.tensor_copy(out=bias_ts[:, 0:2], in_=bm_tanh[:])
-                nc.vector.tensor_copy(out=bias_ts[:, 2:4], in_=bm_sig[:])
-            if 2 <= tick and tick + 2 < N_CH:
-                x_quant(tick + 2)
+                for q, factor in enumerate((lane_unscale[:], lane_half[:])):
+                    nc.vector.tensor_scalar(out=g_grp[:, q, :, :], in0=g_raw[:, q, :, :].rearrange("p t o -> p o t"),
+                                            scalar1=factor, scalar2=None, op0=ALU.mult)
+                nc.vector.tensor_scalar(out=bias_ts[:], in0=bm_ts[:], scalar1=lane_half[:], scalar2=None, op0=ALU.mult)
             if quantised < todo - 1:
                 quant(quantised, 0, CH)
                 quantised += 1

from contextlib import ExitStack

import concourse.mybir as mybir
from concourse.masks import make_identity

F32 = mybir.dt.float32
BF16 = mybir.dt.bfloat16
U32 = mybir.dt.uint32
U8 = mybir.dt.uint8
FP8X4 = mybir.dt.float8_e4m3fn_x4
ACT = mybir.ActivationFunctionType
ALU = mybir.AluOpType

P = 128
H = P // 2
N_TOK = 8192
D = 512
N_BRANCH = 1024
N_OUT = 128
CH = 512
N_CH = N_TOK // CH
TPC = CH // P
N_TT = N_TOK // P

FLOPS = 2 * N_TOK * D * N_BRANCH + 2 * N_TOK * N_BRANCH * N_OUT

X_BUFS = 6
RELU_SCALE = 2.0 ** 40
LAG_MM2 = 4
S_EVAC = (0, 1)
V_EVAC = ()
S_OUT = ()
LAST = N_CH - 1
G_TOK = 0
V_SKIP = ()
V_TWO = ()


def tile_kan_t_kernel(tc, x, W, b, agg, out):
    nc = tc.nc
    x_v = x.rearrange("(p i) k -> p i k", i=N_TT)
    out_v = out.rearrange("(p i) o -> p i o", i=N_TT)

    with ExitStack() as ctx:
        keep = ctx.enter_context(tc.tile_pool(name="keep", bufs=1))
        xpool = ctx.enter_context(tc.tile_pool(name="xraw", bufs=X_BUFS))
        gxpool = ctx.enter_context(tc.tile_pool(name="gx", bufs=3))
        cqpool = ctx.enter_context(tc.tile_pool(name="cq", bufs=4))
        gqpool = ctx.enter_context(tc.tile_pool(name="gq", bufs=4))
        ccpool = ctx.enter_context(tc.tile_pool(name="cc", bufs=4))
        opool = ctx.enter_context(tc.tile_pool(name="osb", bufs=8))
        psa = ctx.enter_context(tc.psum_pool(name="psa", bufs=2))
        psh = ctx.enter_context(tc.psum_pool(name="psh", bufs=6))
        ctx.enter_context(tc.manual_schedule())

        x_codes = keep.tile([P, N_TOK], U32, align_bytes=64)
        x_scales = keep.tile([P, N_TOK], U8, align_bytes=64)
        rg_codes = keep.tile([P, N_TOK], U32, align_bytes=64)
        rg_scales = keep.tile([P, N_TOK], U8, align_bytes=64)
        w_raw_relu = keep.tile([P, 4, 256], BF16)
        w_raw_gelu = keep.tile([P, 4, 256], BF16)
        w_raw_tanh = keep.tile([P, 4, 256], BF16)
        w_raw_sig = keep.tile([P, 4, 256], BF16)
        w_grp = keep.tile([P, N_BRANCH, 4], BF16, align_bytes=64)
        w_codes = keep.tile([P, N_BRANCH], U32, align_bytes=64)
        w_scales = keep.tile([P, N_BRANCH], U8, align_bytes=64)
        g_raw = keep.tile([P, 2, 4, N_OUT], BF16)
        g_grp = keep.tile([P, 2, N_OUT, 4], BF16, align_bytes=64)
        g_codes = keep.tile([P, 2, N_OUT], U32, align_bytes=64)
        g_scales = keep.tile([P, 2, N_OUT], U8, align_bytes=64)
        ident_f = keep.tile([P, P], F32)
        bm_rg = keep.tile([P, 4], BF16)
        bm_ts = keep.tile([P, 4], BF16)
        bias_rg = keep.tile([P, 4], F32)
        bias_ts = keep.tile([P, 4], F32)
        lane_scale = keep.tile([P, 1], F32)
        lane_unscale = keep.tile([P, 1], F32)
        lane_half = keep.tile([P, 1], F32)
        lane_add = keep.tile([P, 1], F32)
        warm = keep.tile([P, 2], F32)

        xr = {}
        xts = {}
        gxs = {}
        hs = {}
        cqs = {}
        gqs = {}
        ccs = {}
        ops = {}

        def load_x(c):
            xraw = xpool.tile([P, TPC, D], BF16)
            xr[c] = xraw
            n = 2 if c == 0 else TPC
            for i in range(0, TPC, n):
                nc.sync.dma_start(out=xraw[:, i:i + n, :], in_=x_v[:, TPC * c + i:TPC * c + i + n, :])

        def load_w(w_raw, c0, c1):
            for u in range(2):
                nc.sync.dma_start(
                    out=w_raw[:, 2 * u:2 * u + 2, :],
                    in_=W[256 * u:256 * (u + 1), c0:c1].rearrange("(q e) c -> q e c", e=2),
                )

        def transposes(c):
            x32 = xr[c][:].rearrange("p i k -> p (i k)").bitcast(F32)
            banks = []
            for a in range(2):
                xt = psa.tile([P, 2, 2, P], F32, tag="a")
                for i2 in range(2):
                    for u in range(2):
                        c0 = 256 * (2 * a + i2) + 128 * u
                        nc.tensor.transpose(xt[:, i2, u, :], x32[:, c0:c0 + P], ident_f[:])
                banks.append(xt)
            xts[c] = banks

        def x_evac(c, a):
            if a == 0:
                gx = gxpool.tile([P, CH, 4], BF16, align_bytes=64)
                gxs[c] = gx
            gx32 = gxs[c][:].rearrange("p r t -> p (r t)").bitcast(F32).rearrange("p (r u) -> p r u", u=2)
            dst = gx32[:, 256 * a:256 * (a + 1), :].rearrange("p (i r) u -> p i r u", i=2)
            src = xts[c][a][:].rearrange("p i u r -> p i r u")
            if c in S_EVAC or (a == 0 and c not in V_EVAC):
                nc.scalar.copy(out=dst, in_=src)
            else:
                nc.vector.tensor_copy(out=dst, in_=src)

        def x_quant(c):
            cols = slice(CH * c, CH * (c + 1))
            nc.vector.quantize_mx(
                out=x_codes[:, cols].bitcast(FP8X4),
                scales=x_scales[:, cols],
                in_=gxs[c][:].rearrange("p r t -> p (r t)"),
            )

        def w_regroup(w_raw, c0, half, factor):
            nc.vector.tensor_scalar(
                out=w_grp[:, c0:c0 + 512, :].rearrange("p (t h m) k -> p h t m k", t=4, h=2)[:, half, :, :, :],
                in0=w_raw[:].rearrange("p k (m t) -> p t m k", t=4),
                scalar1=factor,
                scalar2=None,
                op0=ALU.mult,
            )

        def w_regroup_rg(half):
            w_regroup(w_raw_gelu if half else w_raw_relu, 0, half, 1.0 if half else RELU_SCALE)

        def w_regroup_ts(half):
            w_regroup(w_raw_sig if half else w_raw_tanh, 512, half, 0.5 if half else 1.0)

        def w_quant(j):
            cols = slice(256 * j, 256 * (j + 1))
            nc.vector.quantize_mx(
                out=w_codes[:, cols].bitcast(FP8X4),
                scales=w_scales[:, cols],
                in_=w_grp[:, cols, :].rearrange("p c t -> p (c t)"),
            )

        def first_matmuls(tick):
            c = tick % N_CH
            m0 = 0 if tick < N_CH else 4
            banks = []
            for m in range(m0, m0 + 4):
                h = psh.tile([P, CH], F32, tag="h")
                nc.tensor.matmul_mx(
                    out=h[:],
                    lhsT=w_codes[:, P * m:P * (m + 1)].bitcast(FP8X4),
                    lhsT_scale=w_scales[:, P * m:P * (m + 1)],
                    rhs=x_codes[:, CH * c:CH * (c + 1)].bitcast(FP8X4),
                    rhs_scale=x_scales[:, CH * c:CH * (c + 1)],
                    start=True,
                    stop=True,
                )
                banks.append(h)
            hs[tick] = banks

        def activation(tick, t, lo=0, hi=CH):
            dst = cqs[tick][:, t, lo:hi]
            src = hs[tick][t][:, lo:hi]
            if tick < N_CH:
                nc.scalar.activation(out=dst, in_=src, func=ACT.Gelu, bias=bias_rg[:, t:t + 1], scale=1.0)
            else:
                nc.scalar.activation(out=dst, in_=src, func=ACT.Tanh, bias=bias_ts[:, t:t + 1], scale=1.0)

        def interleave(tick, lo, hi):
            if lo == 0:
                gq = gqpool.tile([P, CH, 4], BF16, align_bytes=64)
                gqs[tick] = gq
            dst = gqs[tick][:, lo:hi, :].rearrange("p (c i) t -> p c t i", i=4)
            src = cqs[tick][:, :, lo:hi].rearrange("p t (c i) -> p c t i", i=4)
            if tick < N_CH:
                nc.vector.tensor_copy(out=dst, in_=src)
            else:
                nc.vector.tensor_scalar(out=dst, in0=src, scalar1=lane_add[:], scalar2=None, op0=ALU.add)

        def quant(tick, lo, hi):
            if tick < N_CH:
                cols = slice(CH * tick + lo, CH * tick + hi)
                codes, scales = rg_codes[:, cols], rg_scales[:, cols]
            else:
                if lo == 0:
                    c_codes = ccpool.tile([P, CH], U32, align_bytes=64)
                    c_scales = ccpool.tile([P, CH], U8, align_bytes=64)
                    ccs[tick - N_CH] = (c_codes, c_scales)
                c_codes, c_scales = ccs[tick - N_CH]
                codes, scales = c_codes[:, lo:hi], c_scales[:, lo:hi]
            nc.vector.quantize_mx(out=codes.bitcast(FP8X4), scales=scales,
                                  in_=gqs[tick][:, lo:hi, :].rearrange("p r t -> p (r t)"))

        def second_matmuls(c, j0, j1):
            if c < LAST - 3:
                o_ps = psa.tile([P, TPC, N_OUT], F32, tag="a")
            else:
                o_ps = psh.tile([P, TPC, N_OUT], F32, tag="h")
            ops[(c, j0)] = o_ps
            c_codes, c_scales = ccs[c]
            for j in range(j0, j1):
                loc = slice(P * j, P * (j + 1))
                glo = slice(CH * c + P * j, CH * c + P * (j + 1))
                pairs = ((rg_codes[:, glo], rg_scales[:, glo]), (c_codes[:, loc], c_scales[:, loc]))
                for q, (cod, sca) in enumerate(pairs):
                    nc.tensor.matmul_mx(
                        out=o_ps[:, j, :],
                        lhsT=cod.bitcast(FP8X4),
                        lhsT_scale=sca,
                        rhs=g_codes[:, q, :].bitcast(FP8X4),
                        rhs_scale=g_scales[:, q, :],
                        start=(q == 0),
                        stop=(q == 1),
                    )

        def store_out(c, j0, j1, on_scalar):
            o_sb = opool.tile([P, TPC, N_OUT], F32)
            if on_scalar:
                nc.scalar.copy(out=o_sb[:, j0:j1, :], in_=ops[(c, j0)][:, j0:j1, :])
            else:
                nc.vector.tensor_copy(out=o_sb[:, j0:j1, :], in_=ops[(c, j0)][:, j0:j1, :])
            nc.sync.dma_start(out=out_v[:, TPC * c + j0:TPC * c + j1, :], in_=o_sb[:, j0:j1, :])

        nc.scalar.dma_start(out=bm_rg[0:H, :], in_=b[0:256].rearrange("(m t) -> m t", t=4))
        nc.scalar.dma_start(out=bm_rg[H:P, :], in_=b[768:1024].rearrange("(m t) -> m t", t=4))
        nc.gpsimd.memset(warm[:], 0.0)
        load_x(0)
        load_w(w_raw_relu, 0, 256)
        load_x(1)
        load_w(w_raw_gelu, 768, 1024)
        load_x(2)
        load_x(3)
        load_w(w_raw_tanh, 256, 512)
        load_w(w_raw_sig, 512, 768)
        for c in range(4, X_BUFS):
            load_x(c)
        nc.scalar.activation(out=warm[:, 1:2], in_=warm[:, 0:1], func=ACT.Gelu)
        make_identity(nc, ident_f[:])
        nc.gpsimd.memset(lane_scale[0:H, :], RELU_SCALE)
        nc.gpsimd.memset(lane_scale[H:P, :], 1.0)
        nc.gpsimd.memset(lane_unscale[0:H, :], 1.0 / RELU_SCALE)
        nc.gpsimd.memset(lane_unscale[H:P, :], 1.0)
        nc.gpsimd.memset(lane_half[0:H, :], 1.0)
        nc.gpsimd.memset(lane_half[H:P, :], 0.5)
        nc.gpsimd.memset(lane_add[0:H, :], 0.0)
        nc.gpsimd.memset(lane_add[H:P, :], 1.0)
        nc.gpsimd.dma_start(out=bm_ts[0:H, :], in_=b[256:512].rearrange("(m t) -> m t", t=4))
        nc.gpsimd.dma_start(out=bm_ts[H:P, :], in_=b[512:768].rearrange("(m t) -> m t", t=4))
        nc.gpsimd.dma_start(out=g_raw[0:H, 0, :, :], in_=agg[0:256, :].rearrange("(p t) o -> p t o", t=4))
        nc.gpsimd.dma_start(out=g_raw[H:P, 0, :, :], in_=agg[768:1024, :].rearrange("(p t) o -> p t o", t=4))
        nc.gpsimd.dma_start(out=g_raw[0:H, 1, :, :], in_=agg[256:512, :].rearrange("(p t) o -> p t o", t=4))
        nc.gpsimd.dma_start(out=g_raw[H:P, 1, :, :], in_=agg[512:768, :].rearrange("(p t) o -> p t o", t=4))
        transposes(0)
        w_regroup_rg(0)

        todo = 0
        quantised = 0
        for tick in range(-3, 2 * N_CH):
            c2 = tick - N_CH
            if X_BUFS <= tick + 8 < N_CH:
                load_x(tick + 8)
            if 0 <= c2 - LAG_MM2:
                second_matmuls(c2 - LAG_MM2, 0, TPC)
            if 0 <= tick:
                cqs[tick] = cqpool.tile([P, 4, CH], BF16 if tick < N_CH else F32, tag=("cq" if tick < N_CH else "ct"), name="cq")
                if c2 == LAST:
                    for t in range(4):
                        activation(tick, t, 0, CH // 2)
                else:
                    activation(tick, 0)
                    activation(tick, 1)
            if -1 <= tick and tick + 1 < 2 * N_CH:
                first_matmuls(tick + 1)
            if tick + 3 < N_CH:
                x_evac(tick + 3, 0)
                x_evac(tick + 3, 1)
            if 0 <= tick:
                if c2 == LAST:
                    for t in range(4):
                        activation(tick, t, CH // 2, CH)
                else:
                    activation(tick, 2)
                    activation(tick, 3)
            if 0 <= c2 - LAG_MM2 - 1:
                store_out(c2 - LAG_MM2 - 1, 0, TPC, c2 - LAG_MM2 - 1 in S_OUT)
            if 0 <= tick + 2 < N_CH:
                x_quant(tick + 2)
            if tick == -2:
                w_regroup_rg(1)
                w_quant(0)
                w_quant(1)
                nc.vector.tensor_scalar(out=bias_rg[:], in0=bm_rg[:], scalar1=lane_scale[:, 0:1], scalar2=None, op0=ALU.mult)
            for k in range(0 if tick < 2 or tick in V_SKIP else 2 if tick in V_TWO else 1):
                interleave(todo, 0, CH)
                if k == 1:
                    quant(quantised, 0, CH)
                    quantised += 1
                todo += 1
            if tick == 0:
                w_regroup_ts(0)
            if tick == 1:
                w_regroup_ts(1)
                w_quant(2)
            if tick == 2:
                w_quant(3)
            if tick == 1:
                for q, factor in enumerate((lane_unscale[:], lane_half[:])):
                    nc.vector.tensor_scalar(out=g_grp[:, q, :, :], in0=g_raw[:, q, :, :].rearrange("p t o -> p o t"),
                                            scalar1=factor, scalar2=None, op0=ALU.mult)
                nc.vector.tensor_scalar(out=bias_ts[:], in0=bm_ts[:], scalar1=lane_half[:], scalar2=None, op0=ALU.mult)
            if quantised < todo - 1:
                quant(quantised, 0, CH)
                quantised += 1
            if tick == 2:
                for q in range(2):
                    nc.vector.quantize_mx(out=g_codes[:, q, :].bitcast(FP8X4), scales=g_scales[:, q, :],
                                          in_=g_grp[:, q, :, :].rearrange("p o t -> p (o t)"))
            if tick + 4 < N_CH:
                transposes(tick + 4)

        end = 2 * N_CH - 1
        interleave(end - 1, 0, CH)
        quant(end - 2, 0, CH)
        interleave(end, 0, CH // 2)
        second_matmuls(LAST - 3, 0, TPC)
        second_matmuls(LAST - 2, 0, TPC)
        quant(end - 1, 0, CH)
        interleave(end, CH // 2, CH)
        quant(end, 0, CH // 2)
        quant(end, CH // 2, CH)
        second_matmuls(LAST - 1, 0, TPC)
        second_matmuls(LAST, 0, TPC // 2)
        second_matmuls(LAST, TPC // 2, TPC)
        for c in range(LAST - 4, LAST):
            store_out(c, 0, TPC, True)
        store_out(LAST, 0, TPC // 2, True)
        store_out(LAST, TPC // 2, TPC, False)
